import numpy as np
import ml_dtypes


def mxq(x, axis, fmt="e4m3"):
    dtype, down = {"e4m3": (ml_dtypes.float8_e4m3fn, 7), "e5m2": (ml_dtypes.float8_e5m2, 14)}[fmt]
    v = np.moveaxis(np.asarray(x, np.float32).astype(ml_dtypes.bfloat16).astype(np.float64), axis, -1)
    blocks = v.reshape(v.shape[:-1] + (-1, 32))
    amax = np.abs(blocks).max(-1, keepdims=True)
    byte = np.maximum(np.where(amax > 0, np.frexp(amax)[1] - 1 + 127, 0) - down, 1)
    scale = np.exp2(byte - 127.0)
    codes = (blocks / scale).astype(np.float32).astype(dtype).astype(np.float64)
    return np.moveaxis((codes * scale).reshape(v.shape), -1, axis)


WIDE = False


def mx_kscale(k):
    if not WIDE:
        return np.ones(k)
    levels = np.array([10, -10, 5, -5, 0])
    a = np.random.permutation(np.resize(levels, k // 512 * 4)).reshape(k // 512, 4)
    idx = np.arange(k)
    return np.exp2(a[idx // 512, idx % 128 // 32])


BF16 = ml_dtypes.bfloat16


def bf(x):
    return np.asarray(x, np.float32).astype(BF16)


def f64(x):
    return np.asarray(x).astype(np.float64)


B, C, H, W, S = 2, 512, 128, 64, 4
NB = (H // S) * (W // S)


def setup_inputs():
    s = mx_kscale(C)
    return {"x": bf(np.random.standard_normal((B, C, H, W)) * s[None, :, None, None]),
            "Wq": bf(np.random.standard_normal((C, C)) * 1.2 * S / np.sqrt(C) / s[None, :]),
            "bq": bf(np.random.standard_normal(C) * 0.3),
            "Wk": bf(np.random.standard_normal((C, C)) * 1.2 * S / np.sqrt(C) / s[None, :]),
            "bk": bf(np.random.standard_normal(C) * 0.3)}


def reference(x, Wq, bq, Wk, bk):
    x_avg = f64(x).reshape(B, C, H // S, S, W // S, S).mean(axis=(3, 5))
    x_avg = x_avg.reshape(B, C, NB).transpose(0, 2, 1)
    xq = mxq(x_avg, 2, "e4m3")
    Q = (xq @ mxq(f64(Wq), 1, "e4m3").T) + f64(bq)
    K = (xq @ mxq(f64(Wk), 1, "e4m3").T) + f64(bk)
    return Q, K

@@ -1,0 +1,177 @@
+from contextlib import ExitStack
+
+import concourse.mybir as mybir
+from concourse.masks import make_identity
+
+FP8X4 = mybir.dt.float8_e4m3fn_x4
+BF16 = mybir.dt.bfloat16
+F32 = mybir.dt.float32
+U32 = mybir.dt.uint32
+U8 = mybir.dt.uint8
+
+B, C, H, W, S = 2, 512, 128, 64, 4
+P = 128
+PACK = 4
+BLOCKS_W = W // S
+N_TILE = P
+ROWS_TILE = N_TILE // BLOCKS_W
+PIXELS_TILE = N_TILE * S * S
+TILES = (H // S) * BLOCKS_W // N_TILE
+O_GROUPS = C // P
+PIXELS_ROW = BLOCKS_W * S * S
+VECTOR_ROWS = 5
+TENSOR_ROWS = ROWS_TILE - VECTOR_ROWS
+HALVES = PIXELS_ROW // P
+
+FLOPS = 2 * 2 * B * (H // S) * BLOCKS_W * C * C
+
+
+def quantise_weight(nc, keep, psum_w, w, ident, which):
+    w_rows = keep.tile([P, O_GROUPS, C], BF16, name="w_rows_" + which)
+    nc.sync.dma_start(out=w_rows[:], in_=w.rearrange("(g p) c -> p g c", p=P))
+    words = w_rows[:].bitcast(F32).rearrange("p g (q u) -> p g u q", u=2)
+    grouped = keep.tile([P, C, PACK], BF16, name="w_grouped_" + which, align_bytes=64)
+    grouped_words = grouped[:].bitcast(F32)
+    for half in range(2):
+        turned = psum_w.tile([P, 2, 2 * P], F32, tag="turned")
+        for g in range(2):
+            for u in range(2):
+                nc.tensor.transpose(
+                    turned[:, u, g * P : (g + 1) * P], words[:, 2 * half + g, u, :], ident[:]
+                )
+        nc.scalar.copy(
+            out=grouped_words[:, half * 2 * P : (half + 1) * 2 * P, :],
+            in_=turned[:].rearrange("p u o -> p o u"),
+        )
+    codes = keep.tile([P, C], U32, name="w_codes_" + which, align_bytes=64)
+    scales = keep.tile([P, C], U8, name="w_scales_" + which, align_bytes=64)
+    nc.vector.quantize_mx(
+        out=codes[:].bitcast(FP8X4),
+        scales=scales[:],
+        in_=grouped[:].rearrange("p o t -> p (o t)"),
+    )
+    return codes, scales
+
+
+def tile_coarseblockattention_pa_kernel(tc, x, Wq, bq, Wk, bk, out_0, out_1):
+    nc = tc.nc
+    with ExitStack() as ctx:
+        keep = ctx.enter_context(tc.tile_pool(name="keep", bufs=1))
+        images = ctx.enter_context(tc.tile_pool(name="images", bufs=B * TILES))
+        work = ctx.enter_context(tc.tile_pool(name="work", bufs=3))
+        results = ctx.enter_context(tc.tile_pool(name="results", bufs=6))
+        psum_w = ctx.enter_context(tc.psum_pool(name="psum_w", bufs=2))
+        psum_pool = ctx.enter_context(tc.psum_pool(name="psum_pool", bufs=2))
+        psum_acc = ctx.enter_context(tc.psum_pool(name="psum_acc", bufs=4))
+
+        ident = keep.tile([P, P], F32)
+        make_identity(nc, ident[:])
+        ident_bf = keep.tile([P, P], BF16)
+        make_identity(nc, ident_bf[:])
+        block_of_f32 = keep.tile([P, BLOCKS_W], F32)
+        nc.vector.tensor_reduce(
+            out=block_of_f32[:],
+            in_=ident_bf[:].rearrange("p (i c k) -> p c i k", c=BLOCKS_W, k=S),
+            axis=mybir.AxisListType.XY,
+            op=mybir.AluOpType.add,
+        )
+        block_of = keep.tile([P, BLOCKS_W], BF16)
+        nc.vector.tensor_copy(out=block_of[:], in_=block_of_f32[:])
+
+        x_tiles = []
+        for b in range(B):
+            by_word = x[b].rearrange("(p j) h w -> p j (h w)", j=PACK)
+            for m in range(TILES):
+                xt = images.tile([P, PACK, PIXELS_TILE], BF16)
+                for j in range(PACK):
+                    nc.sync.dma_start(
+                        out=xt[:, j, :],
+                        in_=by_word[:, j, m * PIXELS_TILE : (m + 1) * PIXELS_TILE],
+                    )
+                x_tiles.append(xt)
+                if b == 0 and m == 0:
+                    q_codes, q_scales = quantise_weight(nc, keep, psum_w, Wq, ident, "q")
+                    k_codes, k_scales = quantise_weight(nc, keep, psum_w, Wk, ident, "k")
+                    q_bias = keep.tile([P, C], BF16)
+                    nc.sync.dma_start(out=q_bias[:], in_=bq.partition_broadcast(P))
+                    k_bias = keep.tile([P, C], BF16)
+                    nc.sync.dma_start(out=k_bias[:], in_=bk.partition_broadcast(P))
+
+        projections = (
+            (q_codes, q_scales, q_bias, out_0),
+            (k_codes, k_scales, k_bias, out_1),
+        )
+
+        for b in range(B):
+            for m in range(TILES):
+                xt = x_tiles[b * TILES + m]
+                sums = work.tile([P, VECTOR_ROWS * BLOCKS_W, PACK], F32)
+                for j in range(PACK):
+                    nc.vector.tensor_reduce(
+                        out=sums[:].rearrange("p (r c) j -> p j r c", c=BLOCKS_W)[:, j],
+                        in_=xt[:, j, : VECTOR_ROWS * PIXELS_ROW].rearrange(
+                            "p (r i c k) -> p r c i k", r=VECTOR_ROWS, i=S, c=BLOCKS_W, k=S
+                        ),
+                        axis=mybir.AxisListType.XY,
+                        op=mybir.AluOpType.add,
+                    )
+                pooled = psum_pool.tile([P, TENSOR_ROWS, PACK, BLOCKS_W], F32)
+                for r in range(TENSOR_ROWS):
+                    first = (VECTOR_ROWS + r) * PIXELS_ROW
+                    turned = psum_w.tile([P, PACK, HALVES, P], BF16, tag="turned")
+                    for j in range(PACK):
+                        for h in range(HALVES):
+                            nc.tensor.transpose(
+                                turned[:, j, h, :],
+                                xt[:, j, first + h * P : first + (h + 1) * P],
+                                ident_bf[:],
+                            )
+                    pixels = work.tile([P, PACK, HALVES, P], BF16)
+                    nc.scalar.copy(out=pixels[:], in_=turned[:])
+                    for j in range(PACK):
+                        for h in range(HALVES):
+                            nc.tensor.matmul(
+                                out=pooled[:, r, j, :],
+                                lhsT=pixels[:, j, h, :],
+                                rhs=block_of[:],
+                                start=(h == 0),
+                                stop=(h == HALVES - 1),
+                            )
+                means = work.tile([P, N_TILE, PACK], BF16, align_bytes=64)
+                nc.scalar.activation(
+                    out=means[:, : VECTOR_ROWS * BLOCKS_W, :],
+                    in_=sums[:],
+                    func=mybir.ActivationFunctionType.Copy,
+                    scale=1.0 / (S * S),
+                )
+                nc.scalar.activation(
+                    out=means[:, VECTOR_ROWS * BLOCKS_W :, :].rearrange(
+                        "p (r c) j -> p r c j", c=BLOCKS_W
+                    ),
+                    in_=pooled[:].rearrange("p r j c -> p r c j"),
+                    func=mybir.ActivationFunctionType.Copy,
+                    scale=1.0 / (S * S),
+                )
+                a_codes = work.tile([P, N_TILE], U32, align_bytes=64)
+                a_scales = work.tile([P, N_TILE], U8, align_bytes=64)
+                nc.vector.quantize_mx(
+                    out=a_codes[:].bitcast(FP8X4),
+                    scales=a_scales[:],
+                    in_=means[:].rearrange("p n j -> p (n j)"),
+                )
+                for w_codes, w_scales, bias, out in projections:
+                    acc = psum_acc.tile([P, C], F32)
+                    nc.tensor.matmul_mx(
+                        out=acc[:],
+                        lhsT=a_codes[:].bitcast(FP8X4),
+                        lhsT_scale=a_scales[:],
+                        rhs=w_codes[:].bitcast(FP8X4),
+                        rhs_scale=w_scales[:],
+                        start=True,
+                        stop=True,
+                    )
+                    res = results.tile([P, C], F32)
+                    nc.vector.tensor_tensor(
+                        out=res[:], in0=acc[:], in1=bias[:], op=mybir.AluOpType.add
+                    )
+                    nc.sync.dma_start(out=out[b, m * N_TILE : (m + 1) * N_TILE, :], in_=res[:])

@@ -8,6 +8,8 @@ BF16 = mybir.dt.bfloat16
 F32 = mybir.dt.float32
 U32 = mybir.dt.uint32
 U8 = mybir.dt.uint8
+ADD = mybir.AluOpType.add
+COPY = mybir.ActivationFunctionType.Copy
 
 B, C, H, W, S = 2, 512, 128, 64, 4
 P = 128
@@ -15,25 +17,26 @@ PACK = 4
 BLOCKS_W = W // S
 N_TILE = P
 ROWS_TILE = N_TILE // BLOCKS_W
-PIXELS_TILE = N_TILE * S * S
-TILES = (H // S) * BLOCKS_W // N_TILE
-O_GROUPS = C // P
 PIXELS_ROW = BLOCKS_W * S * S
-VECTOR_ROWS = 5
-TENSOR_ROWS = ROWS_TILE - VECTOR_ROWS
+PIXELS_TILE = ROWS_TILE * PIXELS_ROW
+TILES = (H // S) // ROWS_TILE
+O_GROUPS = C // P
 HALVES = PIXELS_ROW // P
+
+VECTOR_ROWS = 4
+GPSIMD_ROWS = 1
+TENSOR_ROWS = ROWS_TILE - VECTOR_ROWS - GPSIMD_ROWS
+SBUF_ROWS = VECTOR_ROWS + GPSIMD_ROWS
 
 FLOPS = 2 * 2 * B * (H // S) * BLOCKS_W * C * C
 
 
-def quantise_weight(nc, keep, psum_w, w, ident, which):
-    w_rows = keep.tile([P, O_GROUPS, C], BF16, name="w_rows_" + which)
-    nc.sync.dma_start(out=w_rows[:], in_=w.rearrange("(g p) c -> p g c", p=P))
+def turn_weight(nc, keep, psum_turn, w_rows, ident, which):
     words = w_rows[:].bitcast(F32).rearrange("p g (q u) -> p g u q", u=2)
     grouped = keep.tile([P, C, PACK], BF16, name="w_grouped_" + which, align_bytes=64)
     grouped_words = grouped[:].bitcast(F32)
     for half in range(2):
-        turned = psum_w.tile([P, 2, 2 * P], F32, tag="turned")
+        turned = psum_turn.tile([P, 2, 2 * P], F32, tag="turned")
         for g in range(2):
             for u in range(2):
                 nc.tensor.transpose(
@@ -43,26 +46,119 @@ def quantise_weight(nc, keep, psum_w, w, ident, which):
             out=grouped_words[:, half * 2 * P : (half + 1) * 2 * P, :],
             in_=turned[:].rearrange("p u o -> p o u"),
         )
-    codes = keep.tile([P, C], U32, name="w_codes_" + which, align_bytes=64)
-    scales = keep.tile([P, C], U8, name="w_scales_" + which, align_bytes=64)
+    return grouped
+
+
+def quantise(nc, pool, grouped, which):
+    columns = grouped.shape[1]
+    codes = pool.tile([P, columns], U32, name="codes_" + which, align_bytes=64)
+    scales = pool.tile([P, columns], U8, name="scales_" + which, align_bytes=64)
     nc.vector.quantize_mx(
         out=codes[:].bitcast(FP8X4),
         scales=scales[:],
-        in_=grouped[:].rearrange("p o t -> p (o t)"),
+        in_=grouped[:].rearrange("p n t -> p (n t)"),
     )
     return codes, scales
 
 
+def project(nc, psum_acc, a, w, which):
+    acc = psum_acc.tile([P, C], F32, name="acc_" + which)
+    nc.tensor.matmul_mx(
+        out=acc[:],
+        lhsT=a[0][:].bitcast(FP8X4),
+        lhsT_scale=a[1][:],
+        rhs=w[0][:].bitcast(FP8X4),
+        rhs_scale=w[1][:],
+        start=True,
+        stop=True,
+    )
+    return acc
+
+
+def pool_on_vector(nc, xt, sums):
+    for j in range(PACK):
+        nc.vector.tensor_reduce(
+            out=sums[:, : VECTOR_ROWS * BLOCKS_W, j].rearrange("p (r c) -> p r c", c=BLOCKS_W),
+            in_=xt[:, j, : VECTOR_ROWS * PIXELS_ROW].rearrange(
+                "p (r i c k) -> p r c i k", r=VECTOR_ROWS, i=S, c=BLOCKS_W, k=S
+            ),
+            axis=mybir.AxisListType.XY,
+            op=ADD,
+        )
+
+
+def pool_on_gpsimd(nc, work, xt, sums):
+    first = VECTOR_ROWS * PIXELS_ROW
+    runs = xt[:, :, first : first + GPSIMD_ROWS * PIXELS_ROW].rearrange(
+        "p j (r a s) -> p j r a s", a=HALVES, s=P
+    )
+    two_rows = work.tile([P, PACK, GPSIMD_ROWS, 2, W], F32)
+    nc.gpsimd.tensor_tensor(
+        out=two_rows[:].rearrange("p j r a w -> p j r (a w)"),
+        in0=runs[:, :, :, 0, :],
+        in1=runs[:, :, :, 1, :],
+        op=ADD,
+    )
+    one_row = work.tile([P, PACK, GPSIMD_ROWS, W // 2, 2], F32)
+    nc.gpsimd.tensor_tensor(
+        out=one_row[:].rearrange("p j r q e -> p j r (q e)"),
+        in0=two_rows[:, :, :, 0, :],
+        in1=two_rows[:, :, :, 1, :],
+        op=ADD,
+    )
+    pairs = work.tile([P, PACK, GPSIMD_ROWS, BLOCKS_W, 2], F32)
+    nc.gpsimd.tensor_tensor(
+        out=pairs[:].rearrange("p j r c e -> p j r (c e)"),
+        in0=one_row[:, :, :, :, 0],
+        in1=one_row[:, :, :, :, 1],
+        op=ADD,
+    )
+    nc.gpsimd.tensor_tensor(
+        out=sums[:, VECTOR_ROWS * BLOCKS_W :, :].rearrange("p (r c) j -> p j r c", c=BLOCKS_W),
+        in0=pairs[:, :, :, :, 0],
+        in1=pairs[:, :, :, :, 1],
+        op=ADD,
+    )
+
+
+def pool_on_tensor(nc, flip, psum_turn, xt, ident_bf, block_of, pooled):
+    all_pixels = []
+    for r in range(TENSOR_ROWS):
+        first = (SBUF_ROWS + r) * PIXELS_ROW
+        turned = psum_turn.tile([P, PACK, HALVES, P], BF16, tag="turned")
+        for j in range(PACK):
+            for h in range(HALVES):
+                nc.tensor.transpose(
+                    turned[:, j, h, :], xt[:, j, first + h * P : first + (h + 1) * P], ident_bf[:]
+                )
+        pixels = flip.tile([P, PACK, HALVES, P], BF16)
+        nc.scalar.copy(out=pixels[:].bitcast(F32), in_=turned[:].bitcast(F32))
+        all_pixels.append(pixels)
+    for r in range(TENSOR_ROWS):
+        for j in range(PACK):
+            for h in range(HALVES):
+                nc.tensor.matmul(
+                    out=pooled[:, r, j, :],
+                    lhsT=all_pixels[r][:, j, h, :],
+                    rhs=block_of[:],
+                    start=(h == 0),
+                    stop=(h == HALVES - 1),
+                )
+
+
 def tile_coarseblockattention_pa_kernel(tc, x, Wq, bq, Wk, bk, out_0, out_1):
     nc = tc.nc
+    n_tiles = B * TILES
     with ExitStack() as ctx:
         keep = ctx.enter_context(tc.tile_pool(name="keep", bufs=1))
-        images = ctx.enter_context(tc.tile_pool(name="images", bufs=B * TILES))
+        images = ctx.enter_context(tc.tile_pool(name="images", bufs=n_tiles))
         work = ctx.enter_context(tc.tile_pool(name="work", bufs=3))
-        results = ctx.enter_context(tc.tile_pool(name="results", bufs=6))
-        psum_w = ctx.enter_context(tc.psum_pool(name="psum_w", bufs=2))
-        psum_pool = ctx.enter_context(tc.psum_pool(name="psum_pool", bufs=2))
-        psum_acc = ctx.enter_context(tc.psum_pool(name="psum_acc", bufs=4))
+        results = ctx.enter_context(tc.tile_pool(name="results", bufs=n_tiles))
+        flip = ctx.enter_context(tc.tile_pool(name="flip", bufs=TENSOR_ROWS + 1))
+        psum_turn = ctx.enter_context(tc.psum_pool(name="psum_turn", bufs=4))
+        psum_pooled = ctx.enter_context(tc.psum_pool(name="psum_pooled", bufs=2))
+        psum_acc = ctx.enter_context(tc.psum_pool(name="psum_acc", bufs=1))
+        ctx.enter_context(tc.manual_schedule())
 
         ident = keep.tile([P, P], F32)
         make_identity(nc, ident[:])
@@ -73,7 +169,7 @@ def tile_coarseblockattention_pa_kernel(tc, x, Wq, bq, Wk, bk, out_0, out_1):
             out=block_of_f32[:],
             in_=ident_bf[:].rearrange("p (i c k) -> p c i k", c=BLOCKS_W, k=S),
             axis=mybir.AxisListType.XY,
-            op=mybir.AluOpType.add,
+            op=ADD,
         )
         block_of = keep.tile([P, BLOCKS_W], BF16)
         nc.vector.tensor_copy(out=block_of[:], in_=block_of_f32[:])
@@ -90,88 +186,73 @@ def tile_coarseblockattention_pa_kernel(tc, x, Wq, bq, Wk, bk, out_0, out_1):
                     )
                 x_tiles.append(xt)
                 if b == 0 and m == 0:
-                    q_codes, q_scales = quantise_weight(nc, keep, psum_w, Wq, ident, "q")
-                    k_codes, k_scales = quantise_weight(nc, keep, psum_w, Wk, ident, "k")
+                    q_rows = keep.tile([P, O_GROUPS, C], BF16)
+                    nc.sync.dma_start(out=q_rows[:], in_=Wq.rearrange("(g p) c -> p g c", p=P))
+                    k_rows = keep.tile([P, O_GROUPS, C], BF16)
+                    nc.sync.dma_start(out=k_rows[:], in_=Wk.rearrange("(g p) c -> p g c", p=P))
                     q_bias = keep.tile([P, C], BF16)
                     nc.sync.dma_start(out=q_bias[:], in_=bq.partition_broadcast(P))
                     k_bias = keep.tile([P, C], BF16)
                     nc.sync.dma_start(out=k_bias[:], in_=bk.partition_broadcast(P))
 
-        projections = (
-            (q_codes, q_scales, q_bias, out_0),
-            (k_codes, k_scales, k_bias, out_1),
-        )
-
-        for b in range(B):
-            for m in range(TILES):
-                xt = x_tiles[b * TILES + m]
-                sums = work.tile([P, VECTOR_ROWS * BLOCKS_W, PACK], F32)
-                for j in range(PACK):
-                    nc.vector.tensor_reduce(
-                        out=sums[:].rearrange("p (r c) j -> p j r c", c=BLOCKS_W)[:, j],
-                        in_=xt[:, j, : VECTOR_ROWS * PIXELS_ROW].rearrange(
-                            "p (r i c k) -> p r c i k", r=VECTOR_ROWS, i=S, c=BLOCKS_W, k=S
-                        ),
-                        axis=mybir.AxisListType.XY,
-                        op=mybir.AluOpType.add,
-                    )
-                pooled = psum_pool.tile([P, TENSOR_ROWS, PACK, BLOCKS_W], F32)
-                for r in range(TENSOR_ROWS):
-                    first = (VECTOR_ROWS + r) * PIXELS_ROW
-                    turned = psum_w.tile([P, PACK, HALVES, P], BF16, tag="turned")
-                    for j in range(PACK):
-                        for h in range(HALVES):
-                            nc.tensor.transpose(
-                                turned[:, j, h, :],
-                                xt[:, j, first + h * P : first + (h + 1) * P],
-                                ident_bf[:],
-                            )
-                    pixels = work.tile([P, PACK, HALVES, P], BF16)
-                    nc.scalar.copy(out=pixels[:], in_=turned[:])
-                    for j in range(PACK):
-                        for h in range(HALVES):
-                            nc.tensor.matmul(
-                                out=pooled[:, r, j, :],
-                                lhsT=pixels[:, j, h, :],
-                                rhs=block_of[:],
-                                start=(h == 0),
-                                stop=(h == HALVES - 1),
-                            )
+        all_sums = {}
+        all_pooled = {}
+        all_means = {}
+        all_acc = {}
+        for i in range(n_tiles + 2):
+            if 1 <= i <= n_tiles:
+                sums = all_sums[i - 1]
+                pooled = all_pooled[i - 1]
                 means = work.tile([P, N_TILE, PACK], BF16, align_bytes=64)
                 nc.scalar.activation(
-                    out=means[:, : VECTOR_ROWS * BLOCKS_W, :],
-                    in_=sums[:],
-                    func=mybir.ActivationFunctionType.Copy,
-                    scale=1.0 / (S * S),
-                )
-                nc.scalar.activation(
-                    out=means[:, VECTOR_ROWS * BLOCKS_W :, :].rearrange(
+                    out=means[:, SBUF_ROWS * BLOCKS_W :, :].rearrange(
                         "p (r c) j -> p r c j", c=BLOCKS_W
                     ),
                     in_=pooled[:].rearrange("p r j c -> p r c j"),
-                    func=mybir.ActivationFunctionType.Copy,
+                    func=COPY,
                     scale=1.0 / (S * S),
                 )
-                a_codes = work.tile([P, N_TILE], U32, align_bytes=64)
-                a_scales = work.tile([P, N_TILE], U8, align_bytes=64)
-                nc.vector.quantize_mx(
-                    out=a_codes[:].bitcast(FP8X4),
-                    scales=a_scales[:],
-                    in_=means[:].rearrange("p n j -> p (n j)"),
+                nc.scalar.activation(
+                    out=means[:, : SBUF_ROWS * BLOCKS_W, :],
+                    in_=sums[:],
+                    func=COPY,
+                    scale=1.0 / (S * S),
                 )
-                for w_codes, w_scales, bias, out in projections:
-                    acc = psum_acc.tile([P, C], F32)
-                    nc.tensor.matmul_mx(
-                        out=acc[:],
-                        lhsT=a_codes[:].bitcast(FP8X4),
-                        lhsT_scale=a_scales[:],
-                        rhs=w_codes[:].bitcast(FP8X4),
-                        rhs_scale=w_scales[:],
-                        start=True,
-                        stop=True,
-                    )
-                    res = results.tile([P, C], F32)
-                    nc.vector.tensor_tensor(
-                        out=res[:], in0=acc[:], in1=bias[:], op=mybir.AluOpType.add
-                    )
-                    nc.sync.dma_start(out=out[b, m * N_TILE : (m + 1) * N_TILE, :], in_=res[:])
+                all_means[i - 1] = means
+
+            if i < n_tiles:
+                xt = x_tiles[i]
+                sums = work.tile([P, SBUF_ROWS * BLOCKS_W, PACK], F32)
+                pooled = psum_pooled.tile([P, TENSOR_ROWS, PACK, BLOCKS_W], F32)
+                pool_on_vector(nc, xt, sums)
+                pool_on_gpsimd(nc, work, xt, sums)
+                pool_on_tensor(nc, flip, psum_turn, xt, ident_bf, block_of, pooled)
+                all_sums[i] = sums
+                all_pooled[i] = pooled
+
+            if i == 0:
+                q_grouped = turn_weight(nc, keep, psum_turn, q_rows, ident, "q")
+                k_grouped = turn_weight(nc, keep, psum_turn, k_rows, ident, "k")
+
+            if i >= 2:
+                q_acc, k_acc = all_acc[i - 2]
+                b, m = divmod(i - 2, TILES)
+                blocks = slice(m * N_TILE, (m + 1) * N_TILE)
+                q_res = results.tile([P, C], F32)
+                nc.vector.tensor_tensor(out=q_res[:], in0=q_acc[:], in1=q_bias[:], op=ADD)
+                nc.sync.dma_start(out=out_0[b, blocks, :], in_=q_res[:])
+                k_res = results.tile([P, C], F32)
+                nc.scalar.copy(out=k_res[:], in_=k_acc[:])
+                nc.gpsimd.tensor_tensor(out=k_res[:], in0=k_res[:], in1=k_bias[:], op=ADD)
+                nc.sync.dma_start(out=out_1[b, blocks, :], in_=k_res[:])
+
+            if i == 1:
+                q_weight = quantise(nc, keep, q_grouped, "q")
+                k_weight = quantise(nc, keep, k_grouped, "k")
+
+            if 1 <= i <= n_tiles:
+                a = quantise(nc, work, all_means[i - 1], "a")
+                all_acc[i - 1] = (
+                    project(nc, psum_acc, a, q_weight, "q"),
+                    project(nc, psum_acc, a, k_weight, "k"),
+                )

@@ -22,6 +22,7 @@ PIXELS_TILE = ROWS_TILE * PIXELS_ROW
 TILES = (H // S) // ROWS_TILE
 O_GROUPS = C // P
 HALVES = PIXELS_ROW // P
+PAIR = 2
 
 VECTOR_ROWS = 4
 GPSIMD_ROWS = 1
@@ -122,24 +123,27 @@ def pool_on_gpsimd(nc, work, xt, sums):
 
 
 def pool_on_tensor(nc, flip, psum_turn, xt, ident_bf, block_of, pooled):
+    units = [(r, a) for r in range(TENSOR_ROWS) for a in range(PACK // PAIR)]
     all_pixels = []
-    for r in range(TENSOR_ROWS):
+    for r, a in units:
         first = (SBUF_ROWS + r) * PIXELS_ROW
-        turned = psum_turn.tile([P, PACK, HALVES, P], BF16, tag="turned")
-        for j in range(PACK):
+        turned = psum_turn.tile([P, PAIR, HALVES, P], BF16, tag="turned")
+        for e in range(PAIR):
             for h in range(HALVES):
                 nc.tensor.transpose(
-                    turned[:, j, h, :], xt[:, j, first + h * P : first + (h + 1) * P], ident_bf[:]
+                    turned[:, e, h, :],
+                    xt[:, PAIR * a + e, first + h * P : first + (h + 1) * P],
+                    ident_bf[:],
                 )
-        pixels = flip.tile([P, PACK, HALVES, P], BF16)
+        pixels = flip.tile([P, PAIR, HALVES, P], BF16)
         nc.scalar.copy(out=pixels[:].bitcast(F32), in_=turned[:].bitcast(F32))
         all_pixels.append(pixels)
-    for r in range(TENSOR_ROWS):
-        for j in range(PACK):
+    for (r, a), pixels in zip(units, all_pixels):
+        for e in range(PAIR):
             for h in range(HALVES):
                 nc.tensor.matmul(
-                    out=pooled[:, r, j, :],
-                    lhsT=all_pixels[r][:, j, h, :],
+                    out=pooled[:, r, PAIR * a + e, :],
+                    lhsT=pixels[:, e, h, :],
                     rhs=block_of[:],
                     start=(h == 0),
                     stop=(h == HALVES - 1),
@@ -154,7 +158,7 @@ def tile_coarseblockattention_pa_kernel(tc, x, Wq, bq, Wk, bk, out_0, out_1):
         images = ctx.enter_context(tc.tile_pool(name="images", bufs=n_tiles))
         work = ctx.enter_context(tc.tile_pool(name="work", bufs=3))
         results = ctx.enter_context(tc.tile_pool(name="results", bufs=n_tiles))
-        flip = ctx.enter_context(tc.tile_pool(name="flip", bufs=TENSOR_ROWS + 1))
+        flip = ctx.enter_context(tc.tile_pool(name="flip", bufs=TENSOR_ROWS * PACK // PAIR + 1))
         psum_turn = ctx.enter_context(tc.psum_pool(name="psum_turn", bufs=4))
         psum_pooled = ctx.enter_context(tc.psum_pool(name="psum_pooled", bufs=2))
         psum_acc = ctx.enter_context(tc.psum_pool(name="psum_acc", bufs=1))

@@ -22,7 +22,6 @@ PIXELS_TILE = ROWS_TILE * PIXELS_ROW
 TILES = (H // S) // ROWS_TILE
 O_GROUPS = C // P
 HALVES = PIXELS_ROW // P
-PAIR = 2
 
 VECTOR_ROWS = 4
 GPSIMD_ROWS = 1
@@ -35,17 +34,15 @@ FLOPS = 2 * 2 * B * (H // S) * BLOCKS_W * C * C
 def turn_weight(nc, keep, psum_turn, w_rows, ident, which):
     words = w_rows[:].bitcast(F32).rearrange("p g (q u) -> p g u q", u=2)
     grouped = keep.tile([P, C, PACK], BF16, name="w_grouped_" + which, align_bytes=64)
-    grouped_words = grouped[:].bitcast(F32)
+    grouped_words = grouped[:].bitcast(F32).rearrange("q (p g) u -> q p g u", g=O_GROUPS)
     for half in range(2):
-        turned = psum_turn.tile([P, 2, 2 * P], F32, tag="turned")
+        turned = psum_turn.tile([P, 2, 2, P], F32, tag="turned")
         for g in range(2):
             for u in range(2):
-                nc.tensor.transpose(
-                    turned[:, u, g * P : (g + 1) * P], words[:, 2 * half + g, u, :], ident[:]
-                )
+                nc.tensor.transpose(turned[:, u, g, :], words[:, 2 * half + g, u, :], ident[:])
         nc.scalar.copy(
-            out=grouped_words[:, half * 2 * P : (half + 1) * 2 * P, :],
-            in_=turned[:].rearrange("p u o -> p o u"),
+            out=grouped_words[:, :, 2 * half : 2 * half + 2, :],
+            in_=turned[:].rearrange("q u g p -> q p g u"),
         )
     return grouped
 
@@ -74,6 +71,22 @@ def project(nc, psum_acc, a, w, which):
         stop=True,
     )
     return acc
+
+
+def spread_biases(nc, keep, psum_turn, bias_rows, ident_bf):
+    runs = 2 * O_GROUPS
+    columns_psum = psum_turn.tile([P, P], BF16, tag="turned")
+    nc.tensor.transpose(columns_psum[:], bias_rows[:], ident_bf[:])
+    columns = keep.tile([P, runs], BF16)
+    nc.scalar.copy(out=columns[:], in_=columns_psum[:, :runs])
+    spread_psum = psum_turn.tile([P, runs, P], BF16, tag="turned")
+    for g in range(runs):
+        nc.tensor.transpose(
+            spread_psum[:, g, :], columns[:, g : g + 1].to_broadcast([P, P]), ident_bf[:]
+        )
+    spread = keep.tile([P, runs, P], BF16)
+    nc.scalar.copy(out=spread[:], in_=spread_psum[:])
+    return spread
 
 
 def pool_on_vector(nc, xt, sums):
@@ -123,27 +136,24 @@ def pool_on_gpsimd(nc, work, xt, sums):
 
 
 def pool_on_tensor(nc, flip, psum_turn, xt, ident_bf, block_of, pooled):
-    units = [(r, a) for r in range(TENSOR_ROWS) for a in range(PACK // PAIR)]
     all_pixels = []
-    for r, a in units:
+    for r in range(TENSOR_ROWS):
         first = (SBUF_ROWS + r) * PIXELS_ROW
-        turned = psum_turn.tile([P, PAIR, HALVES, P], BF16, tag="turned")
-        for e in range(PAIR):
+        turned = psum_turn.tile([P, PACK, HALVES, P], BF16, tag="turned")
+        for j in range(PACK):
             for h in range(HALVES):
                 nc.tensor.transpose(
-                    turned[:, e, h, :],
-                    xt[:, PAIR * a + e, first + h * P : first + (h + 1) * P],
-                    ident_bf[:],
+                    turned[:, j, h, :], xt[:, j, first + h * P : first + (h + 1) * P], ident_bf[:]
                 )
-        pixels = flip.tile([P, PAIR, HALVES, P], BF16)
+        pixels = flip.tile([P, PACK, HALVES, P], BF16)
         nc.scalar.copy(out=pixels[:].bitcast(F32), in_=turned[:].bitcast(F32))
         all_pixels.append(pixels)
-    for (r, a), pixels in zip(units, all_pixels):
-        for e in range(PAIR):
+    for r in range(TENSOR_ROWS):
+        for j in range(PACK):
             for h in range(HALVES):
                 nc.tensor.matmul(
-                    out=pooled[:, r, PAIR * a + e, :],
-                    lhsT=pixels[:, e, h, :],
+                    out=pooled[:, r, j, :],
+                    lhsT=all_pixels[r][:, j, h, :],
                     rhs=block_of[:],
                     start=(h == 0),
                     stop=(h == HALVES - 1),
@@ -158,7 +168,7 @@ def tile_coarseblockattention_pa_kernel(tc, x, Wq, bq, Wk, bk, out_0, out_1):
         images = ctx.enter_context(tc.tile_pool(name="images", bufs=n_tiles))
         work = ctx.enter_context(tc.tile_pool(name="work", bufs=3))
         results = ctx.enter_context(tc.tile_pool(name="results", bufs=n_tiles))
-        flip = ctx.enter_context(tc.tile_pool(name="flip", bufs=TENSOR_ROWS * PACK // PAIR + 1))
+        flip = ctx.enter_context(tc.tile_pool(name="flip", bufs=TENSOR_ROWS + 1))
         psum_turn = ctx.enter_context(tc.psum_pool(name="psum_turn", bufs=4))
         psum_pooled = ctx.enter_context(tc.psum_pool(name="psum_pooled", bufs=2))
         psum_acc = ctx.enter_context(tc.psum_pool(name="psum_acc", bufs=1))
@@ -177,6 +187,8 @@ def tile_coarseblockattention_pa_kernel(tc, x, Wq, bq, Wk, bk, out_0, out_1):
         )
         block_of = keep.tile([P, BLOCKS_W], BF16)
         nc.vector.tensor_copy(out=block_of[:], in_=block_of_f32[:])
+        bias_rows = keep.tile([P, P], BF16)
+        nc.vector.memset(bias_rows[:], 0.0)
 
         x_tiles = []
         for b in range(B):
@@ -191,13 +203,16 @@ def tile_coarseblockattention_pa_kernel(tc, x, Wq, bq, Wk, bk, out_0, out_1):
                 x_tiles.append(xt)
                 if b == 0 and m == 0:
                     q_rows = keep.tile([P, O_GROUPS, C], BF16)
-                    nc.sync.dma_start(out=q_rows[:], in_=Wq.rearrange("(g p) c -> p g c", p=P))
+                    nc.sync.dma_start(out=q_rows[:], in_=Wq.rearrange("(p g) c -> p g c", p=P))
                     k_rows = keep.tile([P, O_GROUPS, C], BF16)
-                    nc.sync.dma_start(out=k_rows[:], in_=Wk.rearrange("(g p) c -> p g c", p=P))
-                    q_bias = keep.tile([P, C], BF16)
-                    nc.sync.dma_start(out=q_bias[:], in_=bq.partition_broadcast(P))
-                    k_bias = keep.tile([P, C], BF16)
-                    nc.sync.dma_start(out=k_bias[:], in_=bk.partition_broadcast(P))
+                    nc.sync.dma_start(out=k_rows[:], in_=Wk.rearrange("(p g) c -> p g c", p=P))
+                    nc.sync.dma_start(
+                        out=bias_rows[:O_GROUPS, :], in_=bq.rearrange("(g o) -> g o", o=P)
+                    )
+                    nc.sync.dma_start(
+                        out=bias_rows[O_GROUPS : 2 * O_GROUPS, :],
+                        in_=bk.rearrange("(g o) -> g o", o=P),
+                    )
 
         all_sums = {}
         all_pooled = {}
@@ -237,17 +252,23 @@ def tile_coarseblockattention_pa_kernel(tc, x, Wq, bq, Wk, bk, out_0, out_1):
             if i == 0:
                 q_grouped = turn_weight(nc, keep, psum_turn, q_rows, ident, "q")
                 k_grouped = turn_weight(nc, keep, psum_turn, k_rows, ident, "k")
+                biases = spread_biases(nc, keep, psum_turn, bias_rows, ident_bf)
+                q_bias = biases[:, :O_GROUPS, :].rearrange("p g o -> p (g o)")
+                k_bias = biases[:, O_GROUPS:, :].rearrange("p g o -> p (g o)")
 
             if i >= 2:
                 q_acc, k_acc = all_acc[i - 2]
                 b, m = divmod(i - 2, TILES)
                 blocks = slice(m * N_TILE, (m + 1) * N_TILE)
                 q_res = results.tile([P, C], F32)
-                nc.vector.tensor_tensor(out=q_res[:], in0=q_acc[:], in1=q_bias[:], op=ADD)
+                nc.vector.tensor_tensor(out=q_res[:], in0=q_acc[:], in1=q_bias, op=ADD)
                 nc.sync.dma_start(out=out_0[b, blocks, :], in_=q_res[:])
                 k_res = results.tile([P, C], F32)
-                nc.scalar.copy(out=k_res[:], in_=k_acc[:])
-                nc.gpsimd.tensor_tensor(out=k_res[:], in0=k_res[:], in1=k_bias[:], op=ADD)
+                if i - 2 == n_tiles - 1:
+                    nc.vector.tensor_tensor(out=k_res[:], in0=k_acc[:], in1=k_bias, op=ADD)
+                else:
+                    nc.scalar.copy(out=k_res[:], in_=k_acc[:])
+                    nc.gpsimd.tensor_tensor(out=k_res[:], in0=k_res[:], in1=k_bias, op=ADD)
                 nc.sync.dma_start(out=out_1[b, blocks, :], in_=k_res[:])
 
             if i == 1:

@@ -26,7 +26,8 @@ HALVES = PIXELS_ROW // P
 VECTOR_ROWS = 4
 GPSIMD_ROWS = 1
 TENSOR_ROWS = ROWS_TILE - VECTOR_ROWS - GPSIMD_ROWS
-SBUF_ROWS = VECTOR_ROWS + GPSIMD_ROWS
+VECTOR_BLOCKS = VECTOR_ROWS * BLOCKS_W
+GPSIMD_BLOCKS = GPSIMD_ROWS * BLOCKS_W
 
 FLOPS = 2 * 2 * B * (H // S) * BLOCKS_W * C * C
 
@@ -45,6 +46,22 @@ def turn_weight(nc, keep, psum_turn, w_rows, ident, which):
             in_=turned[:].rearrange("q u g p -> q p g u"),
         )
     return grouped
+
+
+def spread_biases(nc, keep, psum_turn, bias_rows, ident_bf):
+    runs = 2 * O_GROUPS
+    columns_psum = psum_turn.tile([P, P], BF16, tag="turned")
+    nc.tensor.transpose(columns_psum[:], bias_rows[:], ident_bf[:])
+    columns = keep.tile([P, runs], BF16)
+    nc.scalar.copy(out=columns[:], in_=columns_psum[:, :runs])
+    spread_psum = psum_turn.tile([P, runs, P], BF16, tag="turned")
+    for g in range(runs):
+        nc.tensor.transpose(
+            spread_psum[:, g, :], columns[:, g : g + 1].to_broadcast([P, P]), ident_bf[:]
+        )
+    spread = keep.tile([P, runs, P], BF16)
+    nc.scalar.copy(out=spread[:], in_=spread_psum[:])
+    return spread
 
 
 def quantise(nc, pool, grouped, which):
@@ -73,26 +90,10 @@ def project(nc, psum_acc, a, w, which):
     return acc
 
 
-def spread_biases(nc, keep, psum_turn, bias_rows, ident_bf):
-    runs = 2 * O_GROUPS
-    columns_psum = psum_turn.tile([P, P], BF16, tag="turned")
-    nc.tensor.transpose(columns_psum[:], bias_rows[:], ident_bf[:])
-    columns = keep.tile([P, runs], BF16)
-    nc.scalar.copy(out=columns[:], in_=columns_psum[:, :runs])
-    spread_psum = psum_turn.tile([P, runs, P], BF16, tag="turned")
-    for g in range(runs):
-        nc.tensor.transpose(
-            spread_psum[:, g, :], columns[:, g : g + 1].to_broadcast([P, P]), ident_bf[:]
-        )
-    spread = keep.tile([P, runs, P], BF16)
-    nc.scalar.copy(out=spread[:], in_=spread_psum[:])
-    return spread
-
-
-def pool_on_vector(nc, xt, sums):
-    for j in range(PACK):
+def pool_on_vector(nc, xt, v_sums, planes):
+    for j in planes:
         nc.vector.tensor_reduce(
-            out=sums[:, : VECTOR_ROWS * BLOCKS_W, j].rearrange("p (r c) -> p r c", c=BLOCKS_W),
+            out=v_sums[:, j, :].rearrange("p (r c) -> p r c", c=BLOCKS_W),
             in_=xt[:, j, : VECTOR_ROWS * PIXELS_ROW].rearrange(
                 "p (r i c k) -> p r c i k", r=VECTOR_ROWS, i=S, c=BLOCKS_W, k=S
             ),
@@ -101,7 +102,7 @@ def pool_on_vector(nc, xt, sums):
         )
 
 
-def pool_on_gpsimd(nc, work, xt, sums):
+def pool_on_gpsimd(nc, work, xt, g_sums):
     first = VECTOR_ROWS * PIXELS_ROW
     runs = xt[:, :, first : first + GPSIMD_ROWS * PIXELS_ROW].rearrange(
         "p j (r a s) -> p j r a s", a=HALVES, s=P
@@ -128,17 +129,17 @@ def pool_on_gpsimd(nc, work, xt, sums):
         op=ADD,
     )
     nc.gpsimd.tensor_tensor(
-        out=sums[:, VECTOR_ROWS * BLOCKS_W :, :].rearrange("p (r c) j -> p j r c", c=BLOCKS_W),
+        out=g_sums[:].rearrange("p j (r c) -> p j r c", c=BLOCKS_W),
         in0=pairs[:, :, :, :, 0],
         in1=pairs[:, :, :, :, 1],
         op=ADD,
     )
 
 
-def pool_on_tensor(nc, flip, psum_turn, xt, ident_bf, block_of, pooled):
+def pool_on_tensor(nc, flip, psum_turn, xt, ident_bf, block_of, t_sums):
     all_pixels = []
     for r in range(TENSOR_ROWS):
-        first = (SBUF_ROWS + r) * PIXELS_ROW
+        first = (VECTOR_ROWS + GPSIMD_ROWS + r) * PIXELS_ROW
         turned = psum_turn.tile([P, PACK, HALVES, P], BF16, tag="turned")
         for j in range(PACK):
             for h in range(HALVES):
@@ -152,12 +153,37 @@ def pool_on_tensor(nc, flip, psum_turn, xt, ident_bf, block_of, pooled):
         for j in range(PACK):
             for h in range(HALVES):
                 nc.tensor.matmul(
-                    out=pooled[:, r, j, :],
+                    out=t_sums[:, r, j, :],
                     lhsT=all_pixels[r][:, j, h, :],
                     rhs=block_of[:],
                     start=(h == 0),
                     stop=(h == HALVES - 1),
                 )
+
+
+def take_means(nc, work, v_sums, g_sums, t_sums):
+    means = work.tile([P, N_TILE, PACK], BF16, align_bytes=64)
+    nc.scalar.activation(
+        out=means[:, VECTOR_BLOCKS + GPSIMD_BLOCKS :, :].rearrange(
+            "p (r c) j -> p r c j", c=BLOCKS_W
+        ),
+        in_=t_sums[:].rearrange("p r j c -> p r c j"),
+        func=COPY,
+        scale=1.0 / (S * S),
+    )
+    nc.scalar.activation(
+        out=means[:, VECTOR_BLOCKS : VECTOR_BLOCKS + GPSIMD_BLOCKS, :],
+        in_=g_sums[:].rearrange("p j n -> p n j"),
+        func=COPY,
+        scale=1.0 / (S * S),
+    )
+    nc.scalar.activation(
+        out=means[:, :VECTOR_BLOCKS, :],
+        in_=v_sums[:].rearrange("p j n -> p n j"),
+        func=COPY,
+        scale=1.0 / (S * S),
+    )
+    return means
 
 
 def tile_coarseblockattention_pa_kernel(tc, x, Wq, bq, Wk, bk, out_0, out_1):
@@ -167,10 +193,10 @@ def tile_coarseblockattention_pa_kernel(tc, x, Wq, bq, Wk, bk, out_0, out_1):
         keep = ctx.enter_context(tc.tile_pool(name="keep", bufs=1))
         images = ctx.enter_context(tc.tile_pool(name="images", bufs=n_tiles))
         work = ctx.enter_context(tc.tile_pool(name="work", bufs=3))
-        results = ctx.enter_context(tc.tile_pool(name="results", bufs=n_tiles))
         flip = ctx.enter_context(tc.tile_pool(name="flip", bufs=TENSOR_ROWS + 1))
+        results = ctx.enter_context(tc.tile_pool(name="results", bufs=n_tiles))
         psum_turn = ctx.enter_context(tc.psum_pool(name="psum_turn", bufs=4))
-        psum_pooled = ctx.enter_context(tc.psum_pool(name="psum_pooled", bufs=2))
+        psum_sums = ctx.enter_context(tc.psum_pool(name="psum_sums", bufs=2))
         psum_acc = ctx.enter_context(tc.psum_pool(name="psum_acc", bufs=1))
         ctx.enter_context(tc.manual_schedule())
 
@@ -190,6 +216,14 @@ def tile_coarseblockattention_pa_kernel(tc, x, Wq, bq, Wk, bk, out_0, out_1):
         bias_rows = keep.tile([P, P], BF16)
         nc.vector.memset(bias_rows[:], 0.0)
 
+        q_rows = keep.tile([P, O_GROUPS, C], BF16)
+        nc.sync.dma_start(out=q_rows[:], in_=Wq.rearrange("(p g) c -> p g c", p=P))
+        k_rows = keep.tile([P, O_GROUPS, C], BF16)
+        nc.sync.dma_start(out=k_rows[:], in_=Wk.rearrange("(p g) c -> p g c", p=P))
+        nc.sync.dma_start(out=bias_rows[:O_GROUPS, :], in_=bq.rearrange("(g o) -> g o", o=P))
+        nc.sync.dma_start(
+            out=bias_rows[O_GROUPS : 2 * O_GROUPS, :], in_=bk.rearrange("(g o) -> g o", o=P)
+        )
         x_tiles = []
         for b in range(B):
             by_word = x[b].rearrange("(p j) h w -> p j (h w)", j=PACK)
@@ -201,60 +235,28 @@ def tile_coarseblockattention_pa_kernel(tc, x, Wq, bq, Wk, bk, out_0, out_1):
                         in_=by_word[:, j, m * PIXELS_TILE : (m + 1) * PIXELS_TILE],
                     )
                 x_tiles.append(xt)
-                if b == 0 and m == 0:
-                    q_rows = keep.tile([P, O_GROUPS, C], BF16)
-                    nc.sync.dma_start(out=q_rows[:], in_=Wq.rearrange("(p g) c -> p g c", p=P))
-                    k_rows = keep.tile([P, O_GROUPS, C], BF16)
-                    nc.sync.dma_start(out=k_rows[:], in_=Wk.rearrange("(p g) c -> p g c", p=P))
-                    nc.sync.dma_start(
-                        out=bias_rows[:O_GROUPS, :], in_=bq.rearrange("(g o) -> g o", o=P)
-                    )
-                    nc.sync.dma_start(
-                        out=bias_rows[O_GROUPS : 2 * O_GROUPS, :],
-                        in_=bk.rearrange("(g o) -> g o", o=P),
-                    )
+
+        q_grouped = turn_weight(nc, keep, psum_turn, q_rows, ident, "q")
+        k_grouped = turn_weight(nc, keep, psum_turn, k_rows, ident, "k")
+        biases = spread_biases(nc, keep, psum_turn, bias_rows, ident_bf)
+        q_bias = biases[:, :O_GROUPS, :].rearrange("p g o -> p (g o)")
+        k_bias = biases[:, O_GROUPS:, :].rearrange("p g o -> p (g o)")
 
         all_sums = {}
-        all_pooled = {}
-        all_means = {}
         all_acc = {}
         for i in range(n_tiles + 2):
             if 1 <= i <= n_tiles:
-                sums = all_sums[i - 1]
-                pooled = all_pooled[i - 1]
-                means = work.tile([P, N_TILE, PACK], BF16, align_bytes=64)
-                nc.scalar.activation(
-                    out=means[:, SBUF_ROWS * BLOCKS_W :, :].rearrange(
-                        "p (r c) j -> p r c j", c=BLOCKS_W
-                    ),
-                    in_=pooled[:].rearrange("p r j c -> p r c j"),
-                    func=COPY,
-                    scale=1.0 / (S * S),
-                )
-                nc.scalar.activation(
-                    out=means[:, : SBUF_ROWS * BLOCKS_W, :],
-                    in_=sums[:],
-                    func=COPY,
-                    scale=1.0 / (S * S),
-                )
-                all_means[i - 1] = means
+                means = take_means(nc, work, *all_sums[i - 1])
 
             if i < n_tiles:
                 xt = x_tiles[i]
-                sums = work.tile([P, SBUF_ROWS * BLOCKS_W, PACK], F32)
-                pooled = psum_pooled.tile([P, TENSOR_ROWS, PACK, BLOCKS_W], F32)
-                pool_on_vector(nc, xt, sums)
-                pool_on_gpsimd(nc, work, xt, sums)
-                pool_on_tensor(nc, flip, psum_turn, xt, ident_bf, block_of, pooled)
-                all_sums[i] = sums
-                all_pooled[i] = pooled
-
-            if i == 0:
-                q_grouped = turn_weight(nc, keep, psum_turn, q_rows, ident, "q")
-                k_grouped = turn_weight(nc, keep, psum_turn, k_rows, ident, "k")
-                biases = spread_biases(nc, keep, psum_turn, bias_rows, ident_bf)
-                q_bias = biases[:, :O_GROUPS, :].rearrange("p g o -> p (g o)")
-                k_bias = biases[:, O_GROUPS:, :].rearrange("p g o -> p (g o)")
+                v_sums = work.tile([P, PACK, VECTOR_BLOCKS], F32)
+                g_sums = work.tile([P, PACK, GPSIMD_BLOCKS], F32)
+                t_sums = psum_sums.tile([P, TENSOR_ROWS, PACK, BLOCKS_W], F32)
+                all_sums[i] = (v_sums, g_sums, t_sums)
+                pool_on_vector(nc, xt, v_sums, range(PACK // 2))
+                pool_on_gpsimd(nc, work, xt, g_sums)
+                pool_on_tensor(nc, flip, psum_turn, xt, ident_bf, block_of, t_sums)
 
             if i >= 2:
                 q_acc, k_acc = all_acc[i - 2]
@@ -276,8 +278,11 @@ def tile_coarseblockattention_pa_kernel(tc, x, Wq, bq, Wk, bk, out_0, out_1):
                 k_weight = quantise(nc, keep, k_grouped, "k")
 
             if 1 <= i <= n_tiles:
-                a = quantise(nc, work, all_means[i - 1], "a")
+                a = quantise(nc, work, means, "a")
                 all_acc[i - 1] = (
                     project(nc, psum_acc, a, q_weight, "q"),
                     project(nc, psum_acc, a, k_weight, "k"),
                 )
+
+            if i < n_tiles:
+                pool_on_vector(nc, xt, v_sums, range(PACK // 2, PACK))

@@ -9,6 +9,7 @@ F32 = mybir.dt.float32
 U32 = mybir.dt.uint32
 U8 = mybir.dt.uint8
 ADD = mybir.AluOpType.add
+MULT = mybir.AluOpType.mult
 COPY = mybir.ActivationFunctionType.Copy
 
 B, C, H, W, S = 2, 512, 128, 64, 4
@@ -90,19 +91,20 @@ def project(nc, psum_acc, a, w, which):
     return acc
 
 
-def pool_on_vector(nc, xt, v_sums, planes):
-    for j in planes:
-        nc.vector.tensor_reduce(
-            out=v_sums[:, j, :].rearrange("p (r c) -> p r c", c=BLOCKS_W),
-            in_=xt[:, j, : VECTOR_ROWS * PIXELS_ROW].rearrange(
-                "p (r i c k) -> p r c i k", r=VECTOR_ROWS, i=S, c=BLOCKS_W, k=S
-            ),
-            axis=mybir.AxisListType.XY,
-            op=ADD,
-        )
+def pool_on_vector(nc, xt, pooled, planes):
+    with nc.allow_low_precision(reason="the engine adds in float32; only the result is bfloat16"):
+        for j in planes:
+            nc.vector.tensor_reduce(
+                out=pooled[:, :VECTOR_BLOCKS, j].rearrange("p (r c) -> p r c", c=BLOCKS_W),
+                in_=xt[:, j, : VECTOR_ROWS * PIXELS_ROW].rearrange(
+                    "p (r i c k) -> p r c i k", r=VECTOR_ROWS, i=S, c=BLOCKS_W, k=S
+                ),
+                axis=mybir.AxisListType.XY,
+                op=ADD,
+            )
 
 
-def pool_on_gpsimd(nc, work, xt, g_sums):
+def pool_on_gpsimd(nc, work, xt, pooled):
     first = VECTOR_ROWS * PIXELS_ROW
     runs = xt[:, :, first : first + GPSIMD_ROWS * PIXELS_ROW].rearrange(
         "p j (r a s) -> p j r a s", a=HALVES, s=P
@@ -129,7 +131,9 @@ def pool_on_gpsimd(nc, work, xt, g_sums):
         op=ADD,
     )
     nc.gpsimd.tensor_tensor(
-        out=g_sums[:].rearrange("p j (r c) -> p j r c", c=BLOCKS_W),
+        out=pooled[:, VECTOR_BLOCKS : VECTOR_BLOCKS + GPSIMD_BLOCKS, :].rearrange(
+            "p (r c) j -> p j r c", c=BLOCKS_W
+        ),
         in0=pairs[:, :, :, :, 0],
         in1=pairs[:, :, :, :, 1],
         op=ADD,
@@ -161,29 +165,13 @@ def pool_on_tensor(nc, flip, psum_turn, xt, ident_bf, block_of, t_sums):
                 )
 
 
-def take_means(nc, work, v_sums, g_sums, t_sums):
-    means = work.tile([P, N_TILE, PACK], BF16, align_bytes=64)
-    nc.scalar.activation(
-        out=means[:, VECTOR_BLOCKS + GPSIMD_BLOCKS :, :].rearrange(
+def round_tensor_sums(nc, pooled, t_sums):
+    nc.scalar.copy(
+        out=pooled[:, VECTOR_BLOCKS + GPSIMD_BLOCKS :, :].rearrange(
             "p (r c) j -> p r c j", c=BLOCKS_W
         ),
         in_=t_sums[:].rearrange("p r j c -> p r c j"),
-        func=COPY,
-        scale=1.0 / (S * S),
     )
-    nc.scalar.activation(
-        out=means[:, VECTOR_BLOCKS : VECTOR_BLOCKS + GPSIMD_BLOCKS, :],
-        in_=g_sums[:].rearrange("p j n -> p n j"),
-        func=COPY,
-        scale=1.0 / (S * S),
-    )
-    nc.scalar.activation(
-        out=means[:, :VECTOR_BLOCKS, :],
-        in_=v_sums[:].rearrange("p j n -> p n j"),
-        func=COPY,
-        scale=1.0 / (S * S),
-    )
-    return means
 
 
 def tile_coarseblockattention_pa_kernel(tc, x, Wq, bq, Wk, bk, out_0, out_1):
@@ -246,16 +234,15 @@ def tile_coarseblockattention_pa_kernel(tc, x, Wq, bq, Wk, bk, out_0, out_1):
         all_acc = {}
         for i in range(n_tiles + 2):
             if 1 <= i <= n_tiles:
-                means = take_means(nc, work, *all_sums[i - 1])
+                round_tensor_sums(nc, *all_sums[i - 1])
 
             if i < n_tiles:
                 xt = x_tiles[i]
-                v_sums = work.tile([P, PACK, VECTOR_BLOCKS], F32)
-                g_sums = work.tile([P, PACK, GPSIMD_BLOCKS], F32)
+                pooled = work.tile([P, N_TILE, PACK], BF16, align_bytes=64)
                 t_sums = psum_sums.tile([P, TENSOR_ROWS, PACK, BLOCKS_W], F32)
-                all_sums[i] = (v_sums, g_sums, t_sums)
-                pool_on_vector(nc, xt, v_sums, range(PACK // 2))
-                pool_on_gpsimd(nc, work, xt, g_sums)
+                all_sums[i] = (pooled, t_sums)
+                pool_on_vector(nc, xt, pooled, range(PACK // 2))
+                pool_on_gpsimd(nc, work, xt, pooled)
                 pool_on_tensor(nc, flip, psum_turn, xt, ident_bf, block_of, t_sums)
 
             if i >= 2:
@@ -263,13 +250,22 @@ def tile_coarseblockattention_pa_kernel(tc, x, Wq, bq, Wk, bk, out_0, out_1):
                 b, m = divmod(i - 2, TILES)
                 blocks = slice(m * N_TILE, (m + 1) * N_TILE)
                 q_res = results.tile([P, C], F32)
-                nc.vector.tensor_tensor(out=q_res[:], in0=q_acc[:], in1=q_bias, op=ADD)
+                nc.vector.scalar_tensor_tensor(
+                    out=q_res[:], in0=q_acc[:], scalar=1.0 / (S * S), in1=q_bias, op0=MULT, op1=ADD
+                )
                 nc.sync.dma_start(out=out_0[b, blocks, :], in_=q_res[:])
                 k_res = results.tile([P, C], F32)
                 if i - 2 == n_tiles - 1:
-                    nc.vector.tensor_tensor(out=k_res[:], in0=k_acc[:], in1=k_bias, op=ADD)
+                    nc.vector.scalar_tensor_tensor(
+                        out=k_res[:],
+                        in0=k_acc[:],
+                        scalar=1.0 / (S * S),
+                        in1=k_bias,
+                        op0=MULT,
+                        op1=ADD,
+                    )
                 else:
-                    nc.scalar.copy(out=k_res[:], in_=k_acc[:])
+                    nc.scalar.activation(out=k_res[:], in_=k_acc[:], func=COPY, scale=1.0 / (S * S))
                     nc.gpsimd.tensor_tensor(out=k_res[:], in0=k_res[:], in1=k_bias, op=ADD)
                 nc.sync.dma_start(out=out_1[b, blocks, :], in_=k_res[:])
 
@@ -278,11 +274,11 @@ def tile_coarseblockattention_pa_kernel(tc, x, Wq, bq, Wk, bk, out_0, out_1):
                 k_weight = quantise(nc, keep, k_grouped, "k")
 
             if 1 <= i <= n_tiles:
-                a = quantise(nc, work, means, "a")
+                a = quantise(nc, work, all_sums[i - 1][0], "a")
                 all_acc[i - 1] = (
                     project(nc, psum_acc, a, q_weight, "q"),
                     project(nc, psum_acc, a, k_weight, "k"),
                 )
 
             if i < n_tiles:
-                pool_on_vector(nc, xt, v_sums, range(PACK // 2, PACK))
+                pool_on_vector(nc, xt, pooled, range(PACK // 2, PACK))

@@ -11,6 +11,7 @@ U8 = mybir.dt.uint8
 ADD = mybir.AluOpType.add
 MULT = mybir.AluOpType.mult
 COPY = mybir.ActivationFunctionType.Copy
+IDENTITY = mybir.ActivationFunctionType.Identity
 
 B, C, H, W, S = 2, 512, 128, 64, 4
 P = 128
@@ -24,11 +25,8 @@ TILES = (H // S) // ROWS_TILE
 O_GROUPS = C // P
 HALVES = PIXELS_ROW // P
 
-VECTOR_ROWS = 4
-GPSIMD_ROWS = 1
-TENSOR_ROWS = ROWS_TILE - VECTOR_ROWS - GPSIMD_ROWS
-VECTOR_BLOCKS = VECTOR_ROWS * BLOCKS_W
-GPSIMD_BLOCKS = GPSIMD_ROWS * BLOCKS_W
+SHARES = (4, 1, 3)
+LAST_SHARES = (4, 0, 4)
 
 FLOPS = 2 * 2 * B * (H // S) * BLOCKS_W * C * C
 
@@ -62,7 +60,7 @@ def spread_biases(nc, keep, psum_turn, bias_rows, ident_bf):
         )
     spread = keep.tile([P, runs, P], BF16)
     nc.scalar.copy(out=spread[:], in_=spread_psum[:])
-    return spread
+    return columns, spread
 
 
 def quantise(nc, pool, grouped, which):
@@ -91,39 +89,63 @@ def project(nc, psum_acc, a, w, which):
     return acc
 
 
-def pool_on_vector(nc, xt, pooled, planes):
+def project_turned(nc, psum_acc, a, w, which):
+    acc = psum_acc.tile([P, O_GROUPS, N_TILE], F32, name="acc_" + which)
+    for g in range(O_GROUPS):
+        channels = slice(g * P, (g + 1) * P)
+        nc.tensor.matmul_mx(
+            out=acc[:, g, :],
+            lhsT=w[0][:, channels].bitcast(FP8X4),
+            lhsT_scale=w[1][:, channels],
+            rhs=a[0][:].bitcast(FP8X4),
+            rhs_scale=a[1][:],
+            start=True,
+            stop=True,
+        )
+    return acc
+
+
+def turn_back(nc, psum_turn, k_turned, ident):
+    k_back = psum_turn.tile([P, O_GROUPS, P], F32, tag="turned")
+    for g in range(O_GROUPS):
+        nc.tensor.transpose(k_back[:, g, :], k_turned[:, g, :], ident[:])
+    return k_back
+
+
+def pool_on_vector(nc, xt, pooled, planes, shares):
     with nc.allow_low_precision(reason="the engine adds in float32; only the result is bfloat16"):
         for j in planes:
             nc.vector.tensor_reduce(
-                out=pooled[:, :VECTOR_BLOCKS, j].rearrange("p (r c) -> p r c", c=BLOCKS_W),
-                in_=xt[:, j, : VECTOR_ROWS * PIXELS_ROW].rearrange(
-                    "p (r i c k) -> p r c i k", r=VECTOR_ROWS, i=S, c=BLOCKS_W, k=S
+                out=pooled[:, : shares[0] * BLOCKS_W, j].rearrange("p (r c) -> p r c", c=BLOCKS_W),
+                in_=xt[:, j, : shares[0] * PIXELS_ROW].rearrange(
+                    "p (r i c k) -> p r c i k", r=shares[0], i=S, c=BLOCKS_W, k=S
                 ),
                 axis=mybir.AxisListType.XY,
                 op=ADD,
             )
 
 
-def pool_on_gpsimd(nc, work, xt, pooled):
-    first = VECTOR_ROWS * PIXELS_ROW
-    runs = xt[:, :, first : first + GPSIMD_ROWS * PIXELS_ROW].rearrange(
+def pool_on_gpsimd(nc, work, xt, pooled, shares):
+    before, rows = shares[0], shares[1]
+    first = before * PIXELS_ROW
+    runs = xt[:, :, first : first + rows * PIXELS_ROW].rearrange(
         "p j (r a s) -> p j r a s", a=HALVES, s=P
     )
-    two_rows = work.tile([P, PACK, GPSIMD_ROWS, 2, W], F32)
+    two_rows = work.tile([P, PACK, rows, 2, W], F32)
     nc.gpsimd.tensor_tensor(
         out=two_rows[:].rearrange("p j r a w -> p j r (a w)"),
         in0=runs[:, :, :, 0, :],
         in1=runs[:, :, :, 1, :],
         op=ADD,
     )
-    one_row = work.tile([P, PACK, GPSIMD_ROWS, W // 2, 2], F32)
+    one_row = work.tile([P, PACK, rows, W // 2, 2], F32)
     nc.gpsimd.tensor_tensor(
         out=one_row[:].rearrange("p j r q e -> p j r (q e)"),
         in0=two_rows[:, :, :, 0, :],
         in1=two_rows[:, :, :, 1, :],
         op=ADD,
     )
-    pairs = work.tile([P, PACK, GPSIMD_ROWS, BLOCKS_W, 2], F32)
+    pairs = work.tile([P, PACK, rows, BLOCKS_W, 2], F32)
     nc.gpsimd.tensor_tensor(
         out=pairs[:].rearrange("p j r c e -> p j r (c e)"),
         in0=one_row[:, :, :, :, 0],
@@ -131,7 +153,7 @@ def pool_on_gpsimd(nc, work, xt, pooled):
         op=ADD,
     )
     nc.gpsimd.tensor_tensor(
-        out=pooled[:, VECTOR_BLOCKS : VECTOR_BLOCKS + GPSIMD_BLOCKS, :].rearrange(
+        out=pooled[:, before * BLOCKS_W : (before + rows) * BLOCKS_W, :].rearrange(
             "p (r c) j -> p j r c", c=BLOCKS_W
         ),
         in0=pairs[:, :, :, :, 0],
@@ -140,20 +162,31 @@ def pool_on_gpsimd(nc, work, xt, pooled):
     )
 
 
-def pool_on_tensor(nc, flip, psum_turn, xt, ident_bf, block_of, t_sums):
-    all_pixels = []
-    for r in range(TENSOR_ROWS):
-        first = (VECTOR_ROWS + GPSIMD_ROWS + r) * PIXELS_ROW
+def turn_pixels(nc, psum_turn, xt, ident_bf, shares):
+    banks = []
+    for r in range(shares[2]):
+        first = (shares[0] + shares[1] + r) * PIXELS_ROW
         turned = psum_turn.tile([P, PACK, HALVES, P], BF16, tag="turned")
         for j in range(PACK):
             for h in range(HALVES):
                 nc.tensor.transpose(
                     turned[:, j, h, :], xt[:, j, first + h * P : first + (h + 1) * P], ident_bf[:]
                 )
+        banks.append(turned)
+    return banks
+
+
+def copy_pixels(nc, flip, banks):
+    all_pixels = []
+    for turned in banks:
         pixels = flip.tile([P, PACK, HALVES, P], BF16)
         nc.scalar.copy(out=pixels[:].bitcast(F32), in_=turned[:].bitcast(F32))
         all_pixels.append(pixels)
-    for r in range(TENSOR_ROWS):
+    return all_pixels
+
+
+def add_up_pixels(nc, all_pixels, block_of, t_sums):
+    for r in range(len(all_pixels)):
         for j in range(PACK):
             for h in range(HALVES):
                 nc.tensor.matmul(
@@ -165,9 +198,9 @@ def pool_on_tensor(nc, flip, psum_turn, xt, ident_bf, block_of, t_sums):
                 )
 
 
-def round_tensor_sums(nc, pooled, t_sums):
+def round_tensor_sums(nc, pooled, t_sums, shares):
     nc.scalar.copy(
-        out=pooled[:, VECTOR_BLOCKS + GPSIMD_BLOCKS :, :].rearrange(
+        out=pooled[:, (shares[0] + shares[1]) * BLOCKS_W :, :].rearrange(
             "p (r c) j -> p r c j", c=BLOCKS_W
         ),
         in_=t_sums[:].rearrange("p r j c -> p r c j"),
@@ -181,7 +214,7 @@ def tile_coarseblockattention_pa_kernel(tc, x, Wq, bq, Wk, bk, out_0, out_1):
         keep = ctx.enter_context(tc.tile_pool(name="keep", bufs=1))
         images = ctx.enter_context(tc.tile_pool(name="images", bufs=n_tiles))
         work = ctx.enter_context(tc.tile_pool(name="work", bufs=3))
-        flip = ctx.enter_context(tc.tile_pool(name="flip", bufs=TENSOR_ROWS + 1))
+        flip = ctx.enter_context(tc.tile_pool(name="flip", bufs=LAST_SHARES[2] + 1))
         results = ctx.enter_context(tc.tile_pool(name="results", bufs=n_tiles))
         psum_turn = ctx.enter_context(tc.psum_pool(name="psum_turn", bufs=4))
         psum_sums = ctx.enter_context(tc.psum_pool(name="psum_sums", bufs=2))
@@ -226,48 +259,67 @@ def tile_coarseblockattention_pa_kernel(tc, x, Wq, bq, Wk, bk, out_0, out_1):
 
         q_grouped = turn_weight(nc, keep, psum_turn, q_rows, ident, "q")
         k_grouped = turn_weight(nc, keep, psum_turn, k_rows, ident, "k")
-        biases = spread_biases(nc, keep, psum_turn, bias_rows, ident_bf)
+        bias_columns, biases = spread_biases(nc, keep, psum_turn, bias_rows, ident_bf)
         q_bias = biases[:, :O_GROUPS, :].rearrange("p g o -> p (g o)")
         k_bias = biases[:, O_GROUPS:, :].rearrange("p g o -> p (g o)")
 
+        last = n_tiles - 1
         all_sums = {}
         all_acc = {}
         for i in range(n_tiles + 2):
+            leaving = i - 2
             if 1 <= i <= n_tiles:
                 round_tensor_sums(nc, *all_sums[i - 1])
+            if 0 <= leaving < last:
+                k_acc = all_acc[leaving][1]
+                k_turned = work.tile([P, O_GROUPS, N_TILE], F32)
+                for g in range(O_GROUPS):
+                    nc.scalar.activation(
+                        out=k_turned[:, g, :],
+                        in_=k_acc[:, g, :],
+                        func=IDENTITY,
+                        bias=bias_columns[:, O_GROUPS + g : O_GROUPS + g + 1],
+                        scale=1.0 / (S * S),
+                    )
 
             if i < n_tiles:
                 xt = x_tiles[i]
                 pooled = work.tile([P, N_TILE, PACK], BF16, align_bytes=64)
-                t_sums = psum_sums.tile([P, TENSOR_ROWS, PACK, BLOCKS_W], F32)
-                all_sums[i] = (pooled, t_sums)
-                pool_on_vector(nc, xt, pooled, range(PACK // 2))
-                pool_on_gpsimd(nc, work, xt, pooled)
-                pool_on_tensor(nc, flip, psum_turn, xt, ident_bf, block_of, t_sums)
+                shares = LAST_SHARES if i == last else SHARES
+                t_sums = psum_sums.tile([P, shares[2], PACK, BLOCKS_W], F32)
+                all_sums[i] = (pooled, t_sums, shares)
+                pool_on_vector(nc, xt, pooled, range(PACK // 2), shares)
+                if shares[1] > 0:
+                    pool_on_gpsimd(nc, work, xt, pooled, shares)
+                all_pixels = copy_pixels(nc, flip, turn_pixels(nc, psum_turn, xt, ident_bf, shares))
+            if 0 <= leaving < last and i < n_tiles:
+                k_back = turn_back(nc, psum_turn, k_turned, ident)
+            if i < n_tiles:
+                add_up_pixels(nc, all_pixels, block_of, t_sums)
 
-            if i >= 2:
-                q_acc, k_acc = all_acc[i - 2]
-                b, m = divmod(i - 2, TILES)
+            if leaving >= 0:
+                b, m = divmod(leaving, TILES)
                 blocks = slice(m * N_TILE, (m + 1) * N_TILE)
                 q_res = results.tile([P, C], F32)
-                nc.vector.scalar_tensor_tensor(
-                    out=q_res[:], in0=q_acc[:], scalar=1.0 / (S * S), in1=q_bias, op0=MULT, op1=ADD
-                )
-                nc.sync.dma_start(out=out_0[b, blocks, :], in_=q_res[:])
                 k_res = results.tile([P, C], F32)
-                if i - 2 == n_tiles - 1:
+                if leaving < last - 1:
+                    nc.scalar.activation(
+                        out=q_res[:], in_=all_acc[leaving][0][:], func=COPY, scale=1.0 / (S * S)
+                    )
+                    nc.gpsimd.tensor_tensor(out=q_res[:], in0=q_res[:], in1=q_bias, op=ADD)
+                    nc.scalar.copy(out=k_res[:], in_=k_back[:].rearrange("p g o -> p (g o)"))
+                else:
                     nc.vector.scalar_tensor_tensor(
-                        out=k_res[:],
-                        in0=k_acc[:],
+                        out=q_res[:],
+                        in0=all_acc[leaving][0][:],
                         scalar=1.0 / (S * S),
-                        in1=k_bias,
+                        in1=q_bias,
                         op0=MULT,
                         op1=ADD,
                     )
-                else:
-                    nc.scalar.activation(out=k_res[:], in_=k_acc[:], func=COPY, scale=1.0 / (S * S))
-                    nc.gpsimd.tensor_tensor(out=k_res[:], in0=k_res[:], in1=k_bias, op=ADD)
-                nc.sync.dma_start(out=out_1[b, blocks, :], in_=k_res[:])
+                nc.sync.dma_start(out=out_0[b, blocks, :], in_=q_res[:])
+                if leaving < last - 1:
+                    nc.sync.dma_start(out=out_1[b, blocks, :], in_=k_res[:])
 
             if i == 1:
                 q_weight = quantise(nc, keep, q_grouped, "q")
@@ -277,8 +329,23 @@ def tile_coarseblockattention_pa_kernel(tc, x, Wq, bq, Wk, bk, out_0, out_1):
                 a = quantise(nc, work, all_sums[i - 1][0], "a")
                 all_acc[i - 1] = (
                     project(nc, psum_acc, a, q_weight, "q"),
-                    project(nc, psum_acc, a, k_weight, "k"),
+                    (project if i - 1 == last else project_turned)(nc, psum_acc, a, k_weight, "k"),
                 )
 
+            if leaving == last - 1:
+                k_back = turn_back(nc, psum_turn, k_turned, ident)
+                nc.scalar.copy(out=k_res[:], in_=k_back[:].rearrange("p g o -> p (g o)"))
+                nc.sync.dma_start(out=out_1[b, blocks, :], in_=k_res[:])
+            if leaving == last:
+                nc.vector.scalar_tensor_tensor(
+                    out=k_res[:],
+                    in0=all_acc[leaving][1][:],
+                    scalar=1.0 / (S * S),
+                    in1=k_bias,
+                    op0=MULT,
+                    op1=ADD,
+                )
+                nc.sync.dma_start(out=out_1[b, blocks, :], in_=k_res[:])
+
             if i < n_tiles:
-                pool_on_vector(nc, xt, pooled, range(PACK // 2, PACK))
+                pool_on_vector(nc, xt, pooled, range(PACK // 2, PACK), shares)

@@ -264,88 +264,97 @@ def tile_coarseblockattention_pa_kernel(tc, x, Wq, bq, Wk, bk, out_0, out_1):
         k_bias = biases[:, O_GROUPS:, :].rearrange("p g o -> p (g o)")
 
         last = n_tiles - 1
-        all_sums = {}
-        all_acc = {}
+        pooled_of = {}
+        acc_of = {}
+        res_of = {}
+        turned_of = {}
+        back_of = {}
+
+        def out_rows(out, t):
+            return out[t // TILES, (t % TILES) * N_TILE : (t % TILES + 1) * N_TILE, :]
+
+        def through_vector(t, which):
+            nc.vector.scalar_tensor_tensor(
+                out=res_of[t][which][:],
+                in0=acc_of[t][which][:],
+                scalar=1.0 / (S * S),
+                in1=(q_bias, k_bias)[which],
+                op0=MULT,
+                op1=ADD,
+            )
+            nc.sync.dma_start(out=out_rows((out_0, out_1)[which], t), in_=res_of[t][which][:])
+
+        def k_gets_bias(t):
+            turned_of[t] = work.tile([P, O_GROUPS, N_TILE], F32, name="k_turned")
+            for g in range(O_GROUPS):
+                nc.scalar.activation(
+                    out=turned_of[t][:, g, :],
+                    in_=acc_of[t][1][:, g, :],
+                    func=IDENTITY,
+                    bias=bias_columns[:, O_GROUPS + g : O_GROUPS + g + 1],
+                    scale=1.0 / (S * S),
+                )
+
+        def q_leaves(t):
+            nc.scalar.activation(
+                out=res_of[t][0][:], in_=acc_of[t][0][:], func=COPY, scale=1.0 / (S * S)
+            )
+            nc.gpsimd.tensor_tensor(out=res_of[t][0][:], in0=res_of[t][0][:], in1=q_bias, op=ADD)
+
+        def k_leaves(t):
+            nc.scalar.copy(out=res_of[t][1][:], in_=back_of[t][:].rearrange("p g o -> p (g o)"))
+            nc.sync.dma_start(out=out_rows(out_1, t), in_=res_of[t][1][:])
+
+        def multiply(t):
+            a = quantise(nc, work, pooled_of[t][0], "a")
+            acc_of[t] = (
+                project(nc, psum_acc, a, q_weight, "q"),
+                (project if t >= last - 1 else project_turned)(nc, psum_acc, a, k_weight, "k"),
+            )
+
         for i in range(n_tiles + 2):
             leaving = i - 2
             if 1 <= i <= n_tiles:
-                round_tensor_sums(nc, *all_sums[i - 1])
-            if 0 <= leaving < last:
-                k_acc = all_acc[leaving][1]
-                k_turned = work.tile([P, O_GROUPS, N_TILE], F32)
-                for g in range(O_GROUPS):
-                    nc.scalar.activation(
-                        out=k_turned[:, g, :],
-                        in_=k_acc[:, g, :],
-                        func=IDENTITY,
-                        bias=bias_columns[:, O_GROUPS + g : O_GROUPS + g + 1],
-                        scale=1.0 / (S * S),
-                    )
+                round_tensor_sums(nc, *pooled_of[i - 1])
+            if leaving >= 0:
+                q_res = results.tile([P, C], F32)
+                k_res = results.tile([P, C], F32)
+                res_of[leaving] = (q_res, k_res)
+            if 0 <= leaving < last - 1:
+                k_gets_bias(leaving)
+            if i == last:
+                q_leaves(leaving)
 
             if i < n_tiles:
                 xt = x_tiles[i]
                 pooled = work.tile([P, N_TILE, PACK], BF16, align_bytes=64)
                 shares = LAST_SHARES if i == last else SHARES
                 t_sums = psum_sums.tile([P, shares[2], PACK, BLOCKS_W], F32)
-                all_sums[i] = (pooled, t_sums, shares)
+                pooled_of[i] = (pooled, t_sums, shares)
                 pool_on_vector(nc, xt, pooled, range(PACK // 2), shares)
                 if shares[1] > 0:
                     pool_on_gpsimd(nc, work, xt, pooled, shares)
                 all_pixels = copy_pixels(nc, flip, turn_pixels(nc, psum_turn, xt, ident_bf, shares))
-            if 0 <= leaving < last and i < n_tiles:
-                k_back = turn_back(nc, psum_turn, k_turned, ident)
-            if i < n_tiles:
+                if leaving >= 0:
+                    back_of[leaving] = turn_back(nc, psum_turn, turned_of[leaving], ident)
+                if i == last:
+                    multiply(i - 1)
                 add_up_pixels(nc, all_pixels, block_of, t_sums)
-
-            if leaving >= 0:
-                b, m = divmod(leaving, TILES)
-                blocks = slice(m * N_TILE, (m + 1) * N_TILE)
-                q_res = results.tile([P, C], F32)
-                k_res = results.tile([P, C], F32)
-                if leaving < last - 1:
-                    nc.scalar.activation(
-                        out=q_res[:], in_=all_acc[leaving][0][:], func=COPY, scale=1.0 / (S * S)
-                    )
-                    nc.gpsimd.tensor_tensor(out=q_res[:], in0=q_res[:], in1=q_bias, op=ADD)
-                    nc.scalar.copy(out=k_res[:], in_=k_back[:].rearrange("p g o -> p (g o)"))
-                else:
-                    nc.vector.scalar_tensor_tensor(
-                        out=q_res[:],
-                        in0=all_acc[leaving][0][:],
-                        scalar=1.0 / (S * S),
-                        in1=q_bias,
-                        op0=MULT,
-                        op1=ADD,
-                    )
-                nc.sync.dma_start(out=out_0[b, blocks, :], in_=q_res[:])
-                if leaving < last - 1:
-                    nc.sync.dma_start(out=out_1[b, blocks, :], in_=k_res[:])
-
-            if i == 1:
-                q_weight = quantise(nc, keep, q_grouped, "q")
-                k_weight = quantise(nc, keep, k_grouped, "k")
-
-            if 1 <= i <= n_tiles:
-                a = quantise(nc, work, all_sums[i - 1][0], "a")
-                all_acc[i - 1] = (
-                    project(nc, psum_acc, a, q_weight, "q"),
-                    (project if i - 1 == last else project_turned)(nc, psum_acc, a, k_weight, "k"),
-                )
-
-            if leaving == last - 1:
-                k_back = turn_back(nc, psum_turn, k_turned, ident)
-                nc.scalar.copy(out=k_res[:], in_=k_back[:].rearrange("p g o -> p (g o)"))
-                nc.sync.dma_start(out=out_1[b, blocks, :], in_=k_res[:])
-            if leaving == last:
-                nc.vector.scalar_tensor_tensor(
-                    out=k_res[:],
-                    in0=all_acc[leaving][1][:],
-                    scalar=1.0 / (S * S),
-                    in1=k_bias,
-                    op0=MULT,
-                    op1=ADD,
-                )
-                nc.sync.dma_start(out=out_1[b, blocks, :], in_=k_res[:])
-
-            if i < n_tiles:
+                if leaving >= 0:
+                    if i < last:
+                        q_leaves(leaving)
+                    k_leaves(leaving)
+                    nc.sync.dma_start(out=out_rows(out_0, leaving), in_=res_of[leaving][0][:])
+                if i == 1:
+                    q_weight = quantise(nc, keep, q_grouped, "q")
+                    k_weight = quantise(nc, keep, k_grouped, "k")
+                if 1 <= i < last:
+                    multiply(i - 1)
                 pool_on_vector(nc, xt, pooled, range(PACK // 2, PACK), shares)
+            elif i == n_tiles:
+                through_vector(leaving, 0)
+                through_vector(leaving, 1)
+                multiply(last)
+            else:
+                through_vector(last, 0)
+                through_vector(last, 1)

@@ -27,6 +27,7 @@ HALVES = PIXELS_ROW // P
 
 SHARES = (4, 1, 3)
 LAST_SHARES = (4, 0, 4)
+UNITS_BANK = 8
 
 FLOPS = 2 * 2 * B * (H // S) * BLOCKS_W * C * C
 
@@ -162,40 +163,39 @@ def pool_on_gpsimd(nc, work, xt, pooled, shares):
     )
 
 
+def tensor_units(shares):
+    return [(j, r, h) for j in range(PACK) for r in range(shares[2]) for h in range(HALVES)]
+
+
 def turn_pixels(nc, psum_turn, xt, ident_bf, shares):
     banks = []
-    for r in range(shares[2]):
-        first = (shares[0] + shares[1] + r) * PIXELS_ROW
-        turned = psum_turn.tile([P, PACK, HALVES, P], BF16, tag="turned")
-        for j in range(PACK):
-            for h in range(HALVES):
-                nc.tensor.transpose(
-                    turned[:, j, h, :], xt[:, j, first + h * P : first + (h + 1) * P], ident_bf[:]
-                )
-        banks.append(turned)
+    for u, (j, r, h) in enumerate(tensor_units(shares)):
+        if u % UNITS_BANK == 0:
+            turned = psum_turn.tile([P, UNITS_BANK, P], BF16, tag="turned")
+            banks.append(turned)
+        first = (shares[0] + shares[1] + r) * PIXELS_ROW + h * P
+        nc.tensor.transpose(turned[:, u % UNITS_BANK, :], xt[:, j, first : first + P], ident_bf[:])
     return banks
 
 
 def copy_pixels(nc, flip, banks):
     all_pixels = []
     for turned in banks:
-        pixels = flip.tile([P, PACK, HALVES, P], BF16)
+        pixels = flip.tile([P, UNITS_BANK, P], BF16)
         nc.scalar.copy(out=pixels[:].bitcast(F32), in_=turned[:].bitcast(F32))
         all_pixels.append(pixels)
     return all_pixels
 
 
-def add_up_pixels(nc, all_pixels, block_of, t_sums):
-    for r in range(len(all_pixels)):
-        for j in range(PACK):
-            for h in range(HALVES):
-                nc.tensor.matmul(
-                    out=t_sums[:, r, j, :],
-                    lhsT=all_pixels[r][:, j, h, :],
-                    rhs=block_of[:],
-                    start=(h == 0),
-                    stop=(h == HALVES - 1),
-                )
+def add_up_pixels(nc, all_pixels, shares, block_of, t_sums):
+    for u, (j, r, h) in enumerate(tensor_units(shares)):
+        nc.tensor.matmul(
+            out=t_sums[:, r, j, :],
+            lhsT=all_pixels[u // UNITS_BANK][:, u % UNITS_BANK, :],
+            rhs=block_of[:],
+            start=(h == 0),
+            stop=(h == HALVES - 1),
+        )
 
 
 def round_tensor_sums(nc, pooled, t_sums, shares):
@@ -339,7 +339,7 @@ def tile_coarseblockattention_pa_kernel(tc, x, Wq, bq, Wk, bk, out_0, out_1):
                     back_of[leaving] = turn_back(nc, psum_turn, turned_of[leaving], ident)
                 if i == last:
                     multiply(i - 1)
-                add_up_pixels(nc, all_pixels, block_of, t_sums)
+                add_up_pixels(nc, all_pixels, shares, block_of, t_sums)
                 if leaving >= 0:
                     if i < last:
                         q_leaves(leaving)

@@ -167,9 +167,9 @@ def tensor_units(shares):
     return [(j, r, h) for j in range(PACK) for r in range(shares[2]) for h in range(HALVES)]
 
 
-def turn_pixels(nc, psum_turn, xt, ident_bf, shares):
+def turn_pixels(nc, psum_turn, xt, ident_bf, shares, units):
     banks = []
-    for u, (j, r, h) in enumerate(tensor_units(shares)):
+    for u, (j, r, h) in enumerate(units):
         if u % UNITS_BANK == 0:
             turned = psum_turn.tile([P, UNITS_BANK, P], BF16, tag="turned")
             banks.append(turned)
@@ -187,8 +187,8 @@ def copy_pixels(nc, flip, banks):
     return all_pixels
 
 
-def add_up_pixels(nc, all_pixels, shares, block_of, t_sums):
-    for u, (j, r, h) in enumerate(tensor_units(shares)):
+def add_up_pixels(nc, all_pixels, units, block_of, t_sums):
+    for u, (j, r, h) in enumerate(units):
         nc.tensor.matmul(
             out=t_sums[:, r, j, :],
             lhsT=all_pixels[u // UNITS_BANK][:, u % UNITS_BANK, :],
@@ -312,49 +312,72 @@ def tile_coarseblockattention_pa_kernel(tc, x, Wq, bq, Wk, bk, out_0, out_1):
                 (project if t >= last - 1 else project_turned)(nc, psum_acc, a, k_weight, "k"),
             )
 
-        for i in range(n_tiles + 2):
+        def make_room(t):
+            q_res = results.tile([P, C], F32)
+            k_res = results.tile([P, C], F32)
+            res_of[t] = (q_res, k_res)
+
+        def new_tile(t, shares):
+            pooled = work.tile([P, N_TILE, PACK], BF16, align_bytes=64)
+            t_sums = psum_sums.tile([P, shares[2], PACK, BLOCKS_W], F32)
+            pooled_of[t] = (pooled, t_sums, shares)
+            return pooled, t_sums
+
+        for i in range(last):
             leaving = i - 2
-            if 1 <= i <= n_tiles:
+            if i >= 1:
                 round_tensor_sums(nc, *pooled_of[i - 1])
             if leaving >= 0:
-                q_res = results.tile([P, C], F32)
-                k_res = results.tile([P, C], F32)
-                res_of[leaving] = (q_res, k_res)
-            if 0 <= leaving < last - 1:
+                make_room(leaving)
                 k_gets_bias(leaving)
-            if i == last:
+            xt = x_tiles[i]
+            pooled, t_sums = new_tile(i, SHARES)
+            units = tensor_units(SHARES)
+            pool_on_vector(nc, xt, pooled, range(PACK // 2), SHARES)
+            pool_on_gpsimd(nc, work, xt, pooled, SHARES)
+            all_pixels = copy_pixels(
+                nc, flip, turn_pixels(nc, psum_turn, xt, ident_bf, SHARES, units)
+            )
+            if leaving >= 0:
+                back_of[leaving] = turn_back(nc, psum_turn, turned_of[leaving], ident)
+            add_up_pixels(nc, all_pixels, units, block_of, t_sums)
+            if leaving >= 0:
                 q_leaves(leaving)
+                k_leaves(leaving)
+                nc.sync.dma_start(out=out_rows(out_0, leaving), in_=res_of[leaving][0][:])
+            if i == 1:
+                q_weight = quantise(nc, keep, q_grouped, "q")
+                k_weight = quantise(nc, keep, k_grouped, "k")
+            if i >= 1:
+                multiply(i - 1)
+            pool_on_vector(nc, xt, pooled, range(PACK // 2, PACK), SHARES)
 
-            if i < n_tiles:
-                xt = x_tiles[i]
-                pooled = work.tile([P, N_TILE, PACK], BF16, align_bytes=64)
-                shares = LAST_SHARES if i == last else SHARES
-                t_sums = psum_sums.tile([P, shares[2], PACK, BLOCKS_W], F32)
-                pooled_of[i] = (pooled, t_sums, shares)
-                pool_on_vector(nc, xt, pooled, range(PACK // 2), shares)
-                if shares[1] > 0:
-                    pool_on_gpsimd(nc, work, xt, pooled, shares)
-                all_pixels = copy_pixels(nc, flip, turn_pixels(nc, psum_turn, xt, ident_bf, shares))
-                if leaving >= 0:
-                    back_of[leaving] = turn_back(nc, psum_turn, turned_of[leaving], ident)
-                if i == last:
-                    multiply(i - 1)
-                add_up_pixels(nc, all_pixels, shares, block_of, t_sums)
-                if leaving >= 0:
-                    if i < last:
-                        q_leaves(leaving)
-                    k_leaves(leaving)
-                    nc.sync.dma_start(out=out_rows(out_0, leaving), in_=res_of[leaving][0][:])
-                if i == 1:
-                    q_weight = quantise(nc, keep, q_grouped, "q")
-                    k_weight = quantise(nc, keep, k_grouped, "k")
-                if 1 <= i < last:
-                    multiply(i - 1)
-                pool_on_vector(nc, xt, pooled, range(PACK // 2, PACK), shares)
-            elif i == n_tiles:
-                through_vector(leaving, 0)
-                through_vector(leaving, 1)
-                multiply(last)
-            else:
-                through_vector(last, 0)
-                through_vector(last, 1)
+        leaving = last - 2
+        round_tensor_sums(nc, *pooled_of[last - 1])
+        make_room(leaving)
+        k_gets_bias(leaving)
+        q_leaves(leaving)
+        xt = x_tiles[last]
+        pooled, t_sums = new_tile(last, LAST_SHARES)
+        units = tensor_units(LAST_SHARES)
+        pool_on_vector(nc, xt, pooled, range(PACK // 2), LAST_SHARES)
+        all_pixels = copy_pixels(
+            nc, flip, turn_pixels(nc, psum_turn, xt, ident_bf, LAST_SHARES, units)
+        )
+        back_of[leaving] = turn_back(nc, psum_turn, turned_of[leaving], ident)
+        multiply(last - 1)
+        add_up_pixels(nc, all_pixels, units, block_of, t_sums)
+        k_leaves(leaving)
+        nc.sync.dma_start(out=out_rows(out_0, leaving), in_=res_of[leaving][0][:])
+        pool_on_vector(nc, xt, pooled, range(PACK // 2, PACK), LAST_SHARES)
+
+        make_room(last - 1)
+        make_room(last)
+        round_tensor_sums(nc, *pooled_of[last])
+        through_vector(last - 1, 0)
+        a = quantise(nc, work, pooled, "a")
+        q_acc = project(nc, psum_acc, a, q_weight, "q")
+        through_vector(last - 1, 1)
+        acc_of[last] = (q_acc, project(nc, psum_acc, a, k_weight, "k"))
+        through_vector(last, 0)
+        through_vector(last, 1)

@@ -27,6 +27,7 @@ HALVES = PIXELS_ROW // P
 
 SHARES = (4, 1, 3)
 LAST_SHARES = (4, 0, 4)
+STORE_GROUPS = ((0, 1, 2, 3), (4, 5), (6,), (7,))
 UNITS_BANK = 8
 
 FLOPS = 2 * 2 * B * (H // S) * BLOCKS_W * C * C
@@ -215,7 +216,7 @@ def tile_coarseblockattention_pa_kernel(tc, x, Wq, bq, Wk, bk, out_0, out_1):
         images = ctx.enter_context(tc.tile_pool(name="images", bufs=n_tiles))
         work = ctx.enter_context(tc.tile_pool(name="work", bufs=3))
         flip = ctx.enter_context(tc.tile_pool(name="flip", bufs=LAST_SHARES[2] + 1))
-        results = ctx.enter_context(tc.tile_pool(name="results", bufs=n_tiles))
+        results = ctx.enter_context(tc.tile_pool(name="results", bufs=1))
         psum_turn = ctx.enter_context(tc.psum_pool(name="psum_turn", bufs=4))
         psum_sums = ctx.enter_context(tc.psum_pool(name="psum_sums", bufs=2))
         psum_acc = ctx.enter_context(tc.psum_pool(name="psum_acc", bufs=1))
@@ -270,19 +271,29 @@ def tile_coarseblockattention_pa_kernel(tc, x, Wq, bq, Wk, bk, out_0, out_1):
         turned_of = {}
         back_of = {}
 
-        def out_rows(out, t):
-            return out[t // TILES, (t % TILES) * N_TILE : (t % TILES + 1) * N_TILE, :]
+        group_of = {t: group for group in STORE_GROUPS for t in group}
+        group_res = {}
+
+        def store(t, which):
+            group = group_of[t]
+            if t != group[-1]:
+                return
+            first = (group[0] % TILES) * N_TILE
+            out = (out_0, out_1)[which][t // TILES, first : first + len(group) * N_TILE, :]
+            nc.sync.dma_start(
+                out=out.rearrange("(t n) o -> n t o", n=N_TILE), in_=group_res[group][which][:]
+            )
 
         def through_vector(t, which):
             nc.vector.scalar_tensor_tensor(
-                out=res_of[t][which][:],
+                out=res_of[t][which],
                 in0=acc_of[t][which][:],
                 scalar=1.0 / (S * S),
                 in1=(q_bias, k_bias)[which],
                 op0=MULT,
                 op1=ADD,
             )
-            nc.sync.dma_start(out=out_rows((out_0, out_1)[which], t), in_=res_of[t][which][:])
+            store(t, which)
 
         def k_gets_bias(t):
             turned_of[t] = work.tile([P, O_GROUPS, N_TILE], F32, name="k_turned")
@@ -297,13 +308,13 @@ def tile_coarseblockattention_pa_kernel(tc, x, Wq, bq, Wk, bk, out_0, out_1):
 
         def q_leaves(t):
             nc.scalar.activation(
-                out=res_of[t][0][:], in_=acc_of[t][0][:], func=COPY, scale=1.0 / (S * S)
+                out=res_of[t][0], in_=acc_of[t][0][:], func=COPY, scale=1.0 / (S * S)
             )
-            nc.gpsimd.tensor_tensor(out=res_of[t][0][:], in0=res_of[t][0][:], in1=q_bias, op=ADD)
+            nc.gpsimd.tensor_tensor(out=res_of[t][0], in0=res_of[t][0], in1=q_bias, op=ADD)
 
         def k_leaves(t):
-            nc.scalar.copy(out=res_of[t][1][:], in_=back_of[t][:].rearrange("p g o -> p (g o)"))
-            nc.sync.dma_start(out=out_rows(out_1, t), in_=res_of[t][1][:])
+            nc.scalar.copy(out=res_of[t][1], in_=back_of[t][:].rearrange("p g o -> p (g o)"))
+            store(t, 1)
 
         def multiply(t):
             a = quantise(nc, work, pooled_of[t][0], "a")
@@ -313,9 +324,14 @@ def tile_coarseblockattention_pa_kernel(tc, x, Wq, bq, Wk, bk, out_0, out_1):
             )
 
         def make_room(t):
-            q_res = results.tile([P, C], F32)
-            k_res = results.tile([P, C], F32)
-            res_of[t] = (q_res, k_res)
+            group = group_of[t]
+            if t == group[0]:
+                name = "_" + str(group[0])
+                group_res[group] = (
+                    results.tile([P, len(group), C], F32, name="q_res" + name),
+                    results.tile([P, len(group), C], F32, name="k_res" + name),
+                )
+            res_of[t] = tuple(res[:, t - group[0], :] for res in group_res[group])
 
         def new_tile(t, shares):
             pooled = work.tile([P, N_TILE, PACK], BF16, align_bytes=64)
@@ -344,7 +360,7 @@ def tile_coarseblockattention_pa_kernel(tc, x, Wq, bq, Wk, bk, out_0, out_1):
             if leaving >= 0:
                 q_leaves(leaving)
                 k_leaves(leaving)
-                nc.sync.dma_start(out=out_rows(out_0, leaving), in_=res_of[leaving][0][:])
+                store(leaving, 0)
             if i == 1:
                 q_weight = quantise(nc, keep, q_grouped, "q")
                 k_weight = quantise(nc, keep, k_grouped, "k")
@@ -368,7 +384,7 @@ def tile_coarseblockattention_pa_kernel(tc, x, Wq, bq, Wk, bk, out_0, out_1):
         multiply(last - 1)
         add_up_pixels(nc, all_pixels, units, block_of, t_sums)
         k_leaves(leaving)
-        nc.sync.dma_start(out=out_rows(out_0, leaving), in_=res_of[leaving][0][:])
+        store(leaving, 0)
         pool_on_vector(nc, xt, pooled, range(PACK // 2, PACK), LAST_SHARES)
 
         make_room(last - 1)

@@ -27,7 +27,7 @@ HALVES = PIXELS_ROW // P
 
 SHARES = (4, 1, 3)
 LAST_SHARES = (4, 0, 4)
-STORE_GROUPS = ((0, 1, 2, 3), (4, 5), (6,), (7,))
+STORE_GROUPS = ((0, 1, 2, 3), (4,), (5,), (6,), (7,))
 UNITS_BANK = 8
 
 FLOPS = 2 * 2 * B * (H // S) * BLOCKS_W * C * C

@@ -238,9 +238,9 @@ def tile_coarseblockattention_pa_kernel(tc, x, Wq, bq, Wk, bk, out_0, out_1):
         bias_rows = keep.tile([P, P], BF16)
         nc.vector.memset(bias_rows[:], 0.0)
 
-        q_rows = keep.tile([P, O_GROUPS, C], BF16)
+        q_rows = keep.tile([P, O_GROUPS, C], BF16, align_bytes=256)
         nc.sync.dma_start(out=q_rows[:], in_=Wq.rearrange("(p g) c -> p g c", p=P))
-        k_rows = keep.tile([P, O_GROUPS, C], BF16)
+        k_rows = keep.tile([P, O_GROUPS, C], BF16, align_bytes=256)
         nc.sync.dma_start(out=k_rows[:], in_=Wk.rearrange("(p g) c -> p g c", p=P))
         nc.sync.dma_start(out=bias_rows[:O_GROUPS, :], in_=bq.rearrange("(g o) -> g o", o=P))
         nc.sync.dma_start(
@@ -250,7 +250,7 @@ def tile_coarseblockattention_pa_kernel(tc, x, Wq, bq, Wk, bk, out_0, out_1):
         for b in range(B):
             by_word = x[b].rearrange("(p j) h w -> p j (h w)", j=PACK)
             for m in range(TILES):
-                xt = images.tile([P, PACK, PIXELS_TILE], BF16)
+                xt = images.tile([P, PACK, PIXELS_TILE], BF16, align_bytes=256)
                 for j in range(PACK):
                     nc.sync.dma_start(
                         out=xt[:, j, :],
@@ -328,8 +328,8 @@ def tile_coarseblockattention_pa_kernel(tc, x, Wq, bq, Wk, bk, out_0, out_1):
             if t == group[0]:
                 name = "_" + str(group[0])
                 group_res[group] = (
-                    results.tile([P, len(group), C], F32, name="q_res" + name),
-                    results.tile([P, len(group), C], F32, name="k_res" + name),
+                    results.tile([P, len(group), C], F32, name="q_res" + name, align_bytes=256),
+                    results.tile([P, len(group), C], F32, name="k_res" + name, align_bytes=256),
                 )
             res_of[t] = tuple(res[:, t - group[0], :] for res in group_res[group])
 

from contextlib import ExitStack

import concourse.mybir as mybir
from concourse.masks import make_identity

FP8X4 = mybir.dt.float8_e4m3fn_x4
BF16 = mybir.dt.bfloat16
F32 = mybir.dt.float32
U32 = mybir.dt.uint32
U8 = mybir.dt.uint8
ADD = mybir.AluOpType.add
MULT = mybir.AluOpType.mult
COPY = mybir.ActivationFunctionType.Copy
IDENTITY = mybir.ActivationFunctionType.Identity

B, C, H, W, S = 2, 512, 128, 64, 4
P = 128
PACK = 4
BLOCKS_W = W // S
N_TILE = P
ROWS_TILE = N_TILE // BLOCKS_W
PIXELS_ROW = BLOCKS_W * S * S
PIXELS_TILE = ROWS_TILE * PIXELS_ROW
TILES = (H // S) // ROWS_TILE
O_GROUPS = C // P
HALVES = PIXELS_ROW // P

SHARES = (4, 1, 3)
LAST_SHARES = (4, 0, 4)
STORE_GROUPS = ((0, 1, 2, 3), (4,), (5,), (6,), (7,))
UNITS_BANK = 8

FLOPS = 2 * 2 * B * (H // S) * BLOCKS_W * C * C


def turn_weight(nc, keep, psum_turn, w_rows, ident, which):
    words = w_rows[:].bitcast(F32).rearrange("p g (q u) -> p g u q", u=2)
    grouped = keep.tile([P, C, PACK], BF16, name="w_grouped_" + which, align_bytes=64)
    grouped_words = grouped[:].bitcast(F32).rearrange("q (p g) u -> q p g u", g=O_GROUPS)
    for half in range(2):
        turned = psum_turn.tile([P, 2, 2, P], F32, tag="turned")
        for g in range(2):
            for u in range(2):
                nc.tensor.transpose(turned[:, u, g, :], words[:, 2 * half + g, u, :], ident[:])
        nc.scalar.copy(
            out=grouped_words[:, :, 2 * half : 2 * half + 2, :],
            in_=turned[:].rearrange("q u g p -> q p g u"),
        )
    return grouped


def spread_biases(nc, keep, psum_turn, bias_rows, ident_bf):
    runs = 2 * O_GROUPS
    columns_psum = psum_turn.tile([P, P], BF16, tag="turned")
    nc.tensor.transpose(columns_psum[:], bias_rows[:], ident_bf[:])
    columns = keep.tile([P, runs], BF16)
    nc.scalar.copy(out=columns[:], in_=columns_psum[:, :runs])
    spread_psum = psum_turn.tile([P, runs, P], BF16, tag="turned")
    for g in range(runs):
        nc.tensor.transpose(
            spread_psum[:, g, :], columns[:, g : g + 1].to_broadcast([P, P]), ident_bf[:]
        )
    spread = keep.tile([P, runs, P], BF16)
    nc.scalar.copy(out=spread[:], in_=spread_psum[:])
    return columns, spread


def quantise(nc, pool, grouped, which):
    columns = grouped.shape[1]
    codes = pool.tile([P, columns], U32, name="codes_" + which, align_bytes=64)
    scales = pool.tile([P, columns], U8, name="scales_" + which, align_bytes=64)
    nc.vector.quantize_mx(
        out=codes[:].bitcast(FP8X4),
        scales=scales[:],
        in_=grouped[:].rearrange("p n t -> p (n t)"),
    )
    return codes, scales


def project(nc, psum_acc, a, w, which):
    acc = psum_acc.tile([P, C], F32, name="acc_" + which)
    nc.tensor.matmul_mx(
        out=acc[:],
        lhsT=a[0][:].bitcast(FP8X4),
        lhsT_scale=a[1][:],
        rhs=w[0][:].bitcast(FP8X4),
        rhs_scale=w[1][:],
        start=True,
        stop=True,
    )
    return acc


def project_turned(nc, psum_acc, a, w, which):
    acc = psum_acc.tile([P, O_GROUPS, N_TILE], F32, name="acc_" + which)
    for g in range(O_GROUPS):
        channels = slice(g * P, (g + 1) * P)
        nc.tensor.matmul_mx(
            out=acc[:, g, :],
            lhsT=w[0][:, channels].bitcast(FP8X4),
            lhsT_scale=w[1][:, channels],
            rhs=a[0][:].bitcast(FP8X4),
            rhs_scale=a[1][:],
            start=True,
            stop=True,
        )
    return acc


def turn_back(nc, psum_turn, k_turned, ident):
    k_back = psum_turn.tile([P, O_GROUPS, P], F32, tag="turned")
    for g in range(O_GROUPS):
        nc.tensor.transpose(k_back[:, g, :], k_turned[:, g, :], ident[:])
    return k_back


def pool_on_vector(nc, xt, pooled, planes, shares):
    with nc.allow_low_precision(reason="the engine adds in float32; only the result is bfloat16"):
        for j in planes:
            nc.vector.tensor_reduce(
                out=pooled[:, : shares[0] * BLOCKS_W, j].rearrange("p (r c) -> p r c", c=BLOCKS_W),
                in_=xt[:, j, : shares[0] * PIXELS_ROW].rearrange(
                    "p (r i c k) -> p r c i k", r=shares[0], i=S, c=BLOCKS_W, k=S
                ),
                axis=mybir.AxisListType.XY,
                op=ADD,
            )


def pool_on_gpsimd(nc, work, xt, pooled, shares):
    before, rows = shares[0], shares[1]
    first = before * PIXELS_ROW
    runs = xt[:, :, first : first + rows * PIXELS_ROW].rearrange(
        "p j (r a s) -> p j r a s", a=HALVES, s=P
    )
    two_rows = work.tile([P, PACK, rows, 2, W], F32)
    nc.gpsimd.tensor_tensor(
        out=two_rows[:].rearrange("p j r a w -> p j r (a w)"),
        in0=runs[:, :, :, 0, :],
        in1=runs[:, :, :, 1, :],
        op=ADD,
    )
    one_row = work.tile([P, PACK, rows, W // 2, 2], F32)
    nc.gpsimd.tensor_tensor(
        out=one_row[:].rearrange("p j r q e -> p j r (q e)"),
        in0=two_rows[:, :, :, 0, :],
        in1=two_rows[:, :, :, 1, :],
        op=ADD,
    )
    pairs = work.tile([P, PACK, rows, BLOCKS_W, 2], F32)
    nc.gpsimd.tensor_tensor(
        out=pairs[:].rearrange("p j r c e -> p j r (c e)"),
        in0=one_row[:, :, :, :, 0],
        in1=one_row[:, :, :, :, 1],
        op=ADD,
    )
    nc.gpsimd.tensor_tensor(
        out=pooled[:, before * BLOCKS_W : (before + rows) * BLOCKS_W, :].rearrange(
            "p (r c) j -> p j r c", c=BLOCKS_W
        ),
        in0=pairs[:, :, :, :, 0],
        in1=pairs[:, :, :, :, 1],
        op=ADD,
    )


def tensor_units(shares):
    return [(j, r, h) for j in range(PACK) for r in range(shares[2]) for h in range(HALVES)]


def turn_pixels(nc, psum_turn, xt, ident_bf, shares, units):
    banks = []
    for u, (j, r, h) in enumerate(units):
        if u % UNITS_BANK == 0:
            turned = psum_turn.tile([P, UNITS_BANK, P], BF16, tag="turned")
            banks.append(turned)
        first = (shares[0] + shares[1] + r) * PIXELS_ROW + h * P
        nc.tensor.transpose(turned[:, u % UNITS_BANK, :], xt[:, j, first : first + P], ident_bf[:])
    return banks


def copy_pixels(nc, flip, banks):
    all_pixels = []
    for turned in banks:
        pixels = flip.tile([P, UNITS_BANK, P], BF16)
        nc.scalar.copy(out=pixels[:].bitcast(F32), in_=turned[:].bitcast(F32))
        all_pixels.append(pixels)
    return all_pixels


def add_up_pixels(nc, all_pixels, units, block_of, t_sums):
    for u, (j, r, h) in enumerate(units):
        nc.tensor.matmul(
            out=t_sums[:, r, j, :],
            lhsT=all_pixels[u // UNITS_BANK][:, u % UNITS_BANK, :],
            rhs=block_of[:],
            start=(h == 0),
            stop=(h == HALVES - 1),
        )


def round_tensor_sums(nc, pooled, t_sums, shares):
    nc.scalar.copy(
        out=pooled[:, (shares[0] + shares[1]) * BLOCKS_W :, :].rearrange(
            "p (r c) j -> p r c j", c=BLOCKS_W
        ),
        in_=t_sums[:].rearrange("p r j c -> p r c j"),
    )


def tile_coarseblockattention_pa_kernel(tc, x, Wq, bq, Wk, bk, out_0, out_1):
    nc = tc.nc
    n_tiles = B * TILES
    with ExitStack() as ctx:
        keep = ctx.enter_context(tc.tile_pool(name="keep", bufs=1))
        images = ctx.enter_context(tc.tile_pool(name="images", bufs=n_tiles))
        work = ctx.enter_context(tc.tile_pool(name="work", bufs=3))
        flip = ctx.enter_context(tc.tile_pool(name="flip", bufs=LAST_SHARES[2] + 1))
        results = ctx.enter_context(tc.tile_pool(name="results", bufs=1))
        psum_turn = ctx.enter_context(tc.psum_pool(name="psum_turn", bufs=4))
        psum_sums = ctx.enter_context(tc.psum_pool(name="psum_sums", bufs=2))
        psum_acc = ctx.enter_context(tc.psum_pool(name="psum_acc", bufs=1))
        ctx.enter_context(tc.manual_schedule())

        ident = keep.tile([P, P], F32)
        make_identity(nc, ident[:])
        ident_bf = keep.tile([P, P], BF16)
        make_identity(nc, ident_bf[:])
        block_of_f32 = keep.tile([P, BLOCKS_W], F32)
        nc.vector.tensor_reduce(
            out=block_of_f32[:],
            in_=ident_bf[:].rearrange("p (i c k) -> p c i k", c=BLOCKS_W, k=S),
            axis=mybir.AxisListType.XY,
            op=ADD,
        )
        block_of = keep.tile([P, BLOCKS_W], BF16)
        nc.vector.tensor_copy(out=block_of[:], in_=block_of_f32[:])
        bias_rows = keep.tile([P, P], BF16)
        nc.vector.memset(bias_rows[:], 0.0)

        q_rows = keep.tile([P, O_GROUPS, C], BF16, align_bytes=256)
        nc.sync.dma_start(out=q_rows[:], in_=Wq.rearrange("(p g) c -> p g c", p=P))
        k_rows = keep.tile([P, O_GROUPS, C], BF16, align_bytes=256)
        nc.sync.dma_start(out=k_rows[:], in_=Wk.rearrange("(p g) c -> p g c", p=P))
        nc.sync.dma_start(out=bias_rows[:O_GROUPS, :], in_=bq.rearrange("(g o) -> g o", o=P))
        nc.sync.dma_start(
            out=bias_rows[O_GROUPS : 2 * O_GROUPS, :], in_=bk.rearrange("(g o) -> g o", o=P)
        )
        x_tiles = []
        for b in range(B):
            by_word = x[b].rearrange("(p j) h w -> p j (h w)", j=PACK)
            for m in range(TILES):
                xt = images.tile([P, PACK, PIXELS_TILE], BF16, align_bytes=256)
                for j in range(PACK):
                    nc.sync.dma_start(
                        out=xt[:, j, :],
                        in_=by_word[:, j, m * PIXELS_TILE : (m + 1) * PIXELS_TILE],
                    )
                x_tiles.append(xt)

        q_grouped = turn_weight(nc, keep, psum_turn, q_rows, ident, "q")
        k_grouped = turn_weight(nc, keep, psum_turn, k_rows, ident, "k")
        bias_columns, biases = spread_biases(nc, keep, psum_turn, bias_rows, ident_bf)
        q_bias = biases[:, :O_GROUPS, :].rearrange("p g o -> p (g o)")
        k_bias = biases[:, O_GROUPS:, :].rearrange("p g o -> p (g o)")

        last = n_tiles - 1
        pooled_of = {}
        acc_of = {}
        res_of = {}
        turned_of = {}
        back_of = {}

        group_of = {t: group for group in STORE_GROUPS for t in group}
        group_res = {}

        def store(t, which):
            group = group_of[t]
            if t != group[-1]:
                return
            first = (group[0] % TILES) * N_TILE
            out = (out_0, out_1)[which][t // TILES, first : first + len(group) * N_TILE, :]
            nc.sync.dma_start(
                out=out.rearrange("(t n) o -> n t o", n=N_TILE), in_=group_res[group][which][:]
            )

        def through_vector(t, which):
            nc.vector.scalar_tensor_tensor(
                out=res_of[t][which],
                in0=acc_of[t][which][:],
                scalar=1.0 / (S * S),
                in1=(q_bias, k_bias)[which],
                op0=MULT,
                op1=ADD,
            )
            store(t, which)

        def k_gets_bias(t):
            turned_of[t] = work.tile([P, O_GROUPS, N_TILE], F32, name="k_turned")
            for g in range(O_GROUPS):
                nc.scalar.activation(
                    out=turned_of[t][:, g, :],
                    in_=acc_of[t][1][:, g, :],
                    func=IDENTITY,
                    bias=bias_columns[:, O_GROUPS + g : O_GROUPS + g + 1],
                    scale=1.0 / (S * S),
                )

        def q_leaves(t):
            nc.scalar.activation(
                out=res_of[t][0], in_=acc_of[t][0][:], func=COPY, scale=1.0 / (S * S)
            )
            nc.gpsimd.tensor_tensor(out=res_of[t][0], in0=res_of[t][0], in1=q_bias, op=ADD)

        def k_leaves(t):
            nc.scalar.copy(out=res_of[t][1], in_=back_of[t][:].rearrange("p g o -> p (g o)"))
            store(t, 1)

        def multiply(t):
            a = quantise(nc, work, pooled_of[t][0], "a")
            acc_of[t] = (
                project(nc, psum_acc, a, q_weight, "q"),
                (project if t >= last - 1 else project_turned)(nc, psum_acc, a, k_weight, "k"),
            )

        def make_room(t):
            group = group_of[t]
            if t == group[0]:
                name = "_" + str(group[0])
                group_res[group] = (
                    results.tile([P, len(group), C], F32, name="q_res" + name, align_bytes=256),
                    results.tile([P, len(group), C], F32, name="k_res" + name, align_bytes=256),
                )
            res_of[t] = tuple(res[:, t - group[0], :] for res in group_res[group])

        def new_tile(t, shares):
            pooled = work.tile([P, N_TILE, PACK], BF16, align_bytes=64)
            t_sums = psum_sums.tile([P, shares[2], PACK, BLOCKS_W], F32)
            pooled_of[t] = (pooled, t_sums, shares)
            return pooled, t_sums

        for i in range(last):
            leaving = i - 2
            if i >= 1:
                round_tensor_sums(nc, *pooled_of[i - 1])
            if leaving >= 0:
                make_room(leaving)
                k_gets_bias(leaving)
            xt = x_tiles[i]
            pooled, t_sums = new_tile(i, SHARES)
            units = tensor_units(SHARES)
            pool_on_vector(nc, xt, pooled, range(PACK // 2), SHARES)
            pool_on_gpsimd(nc, work, xt, pooled, SHARES)
            all_pixels = copy_pixels(
                nc, flip, turn_pixels(nc, psum_turn, xt, ident_bf, SHARES, units)
            )
            if leaving >= 0:
                back_of[leaving] = turn_back(nc, psum_turn, turned_of[leaving], ident)
            add_up_pixels(nc, all_pixels, units, block_of, t_sums)
            if leaving >= 0:
                q_leaves(leaving)
                k_leaves(leaving)
                store(leaving, 0)
            if i == 1:
                q_weight = quantise(nc, keep, q_grouped, "q")
                k_weight = quantise(nc, keep, k_grouped, "k")
            if i >= 1:
                multiply(i - 1)
            pool_on_vector(nc, xt, pooled, range(PACK // 2, PACK), SHARES)

        leaving = last - 2
        round_tensor_sums(nc, *pooled_of[last - 1])
        make_room(leaving)
        k_gets_bias(leaving)
        q_leaves(leaving)
        xt = x_tiles[last]
        pooled, t_sums = new_tile(last, LAST_SHARES)
        units = tensor_units(LAST_SHARES)
        pool_on_vector(nc, xt, pooled, range(PACK // 2), LAST_SHARES)
        all_pixels = copy_pixels(
            nc, flip, turn_pixels(nc, psum_turn, xt, ident_bf, LAST_SHARES, units)
        )
        back_of[leaving] = turn_back(nc, psum_turn, turned_of[leaving], ident)
        multiply(last - 1)
        add_up_pixels(nc, all_pixels, units, block_of, t_sums)
        k_leaves(leaving)
        store(leaving, 0)
        pool_on_vector(nc, xt, pooled, range(PACK // 2, PACK), LAST_SHARES)

        make_room(last - 1)
        make_room(last)
        round_tensor_sums(nc, *pooled_of[last])
        through_vector(last - 1, 0)
        a = quantise(nc, work, pooled, "a")
        q_acc = project(nc, psum_acc, a, q_weight, "q")
        through_vector(last - 1, 1)
        acc_of[last] = (q_acc, project(nc, psum_acc, a, k_weight, "k"))
        through_vector(last, 0)
        through_vector(last, 1)
